import numpy as np
import ml_dtypes


def mxq(x, axis, fmt="e4m3"):
    dtype, down = {"e4m3": (ml_dtypes.float8_e4m3fn, 7), "e5m2": (ml_dtypes.float8_e5m2, 14)}[fmt]
    v = np.moveaxis(np.asarray(x, np.float32).astype(ml_dtypes.bfloat16).astype(np.float64), axis, -1)
    blocks = v.reshape(v.shape[:-1] + (-1, 32))
    amax = np.abs(blocks).max(-1, keepdims=True)
    byte = np.maximum(np.where(amax > 0, np.frexp(amax)[1] - 1 + 127, 0) - down, 1)
    scale = np.exp2(byte - 127.0)
    codes = (blocks / scale).astype(np.float32).astype(dtype).astype(np.float64)
    return np.moveaxis((codes * scale).reshape(v.shape), -1, axis)


WIDE = False


def mx_kscale(k):
    if not WIDE:
        return np.ones(k)
    levels = np.array([10, -10, 5, -5, 0])
    a = np.random.permutation(np.resize(levels, k // 512 * 4)).reshape(k // 512, 4)
    idx = np.arange(k)
    return np.exp2(a[idx // 512, idx % 128 // 32])


BF16 = ml_dtypes.bfloat16


def bf(x):
    return np.asarray(x, np.float32).astype(BF16)


def f64(x):
    return np.asarray(x).astype(np.float64)


D, HIST, HID, N, B = 256, 8, 512, 32, 128
FMIN, FMAX = 0.5, 40.0
TICK_INTERVAL = 0.1
LN_EPS = 1e-5
ERF_CUT, ERF_TERMS = 6.0, 110


def erf(v):
    a = np.clip(v, -ERF_CUT, ERF_CUT)
    u = 2.0 * a * a
    acc = np.ones_like(a)
    for k in range(ERF_TERMS, 0, -1):
        acc *= u
        acc /= 2.0 * k + 1.0
        acc += 1.0
    return 2.0 / np.sqrt(np.pi) * a * np.exp(-a * a) * acc


def gelu(v):
    return 0.5 * v * (1.0 + erf(v / np.sqrt(2.0)))


def oscillator(tick):
    i = np.arange(N, dtype=np.float64)
    freq = FMIN * (FMAX / FMIN) ** (i / (N - 1))
    phase = np.mod(i * 2.3571, 2.0 * np.pi)
    t = tick * TICK_INTERVAL
    return 1.0 + 0.5 * np.sin(2.0 * np.pi * freq * t + phase)


def setup_inputs():
    s = mx_kscale(HID)
    return {"h1": bf(gelu(np.random.standard_normal((B, N, HID))) * s),
            "W2": bf(np.random.standard_normal((N, HID, HID)) * 0.8 / np.sqrt(HID) / s[:, None]),
            "b2": bf(np.random.standard_normal((N, HID)) * 0.25),
            "W3": bf(np.random.standard_normal((N, HID, D)) * 1.5 / np.sqrt(HID)),
            "b3": bf(np.random.standard_normal((N, D)) * 0.3),
            "gamma": bf(1.0 + 0.1 * np.random.standard_normal((N, D))),
            "beta": bf(np.random.standard_normal((N, D)) * 0.3),
            "tick": 7}


def reference(h1, W2, b2, W3, b3, gamma, beta, tick):
    a = f64(h1).transpose(1, 0, 2)
    g = gelu((mxq(a, 2, "e4m3") @ mxq(f64(W2), 1, "e4m3")) + f64(b2)[:, None, :])
    y = (mxq(g, 2, "e4m3") @ mxq(f64(W3), 1, "e4m3")) + f64(b3)[:, None, :]
    mu = y.mean(-1, keepdims=True)
    var = ((y - mu) ** 2).mean(-1, keepdims=True)
    z = (y - mu) / np.sqrt(var + LN_EPS) * f64(gamma)[:, None, :] + f64(beta)[:, None, :]
    return (z * oscillator(tick)[:, None, None]).transpose(1, 0, 2)

@@ -1,0 +1,248 @@
+from contextlib import ExitStack
+
+import concourse.mybir as mybir
+from concourse.masks import make_identity
+
+FP8X4 = mybir.dt.float8_e4m3fn_x4
+BF16 = mybir.dt.bfloat16
+F32 = mybir.dt.float32
+U32 = mybir.dt.uint32
+U8 = mybir.dt.uint8
+ALU = mybir.AluOpType
+ACT = mybir.ActivationFunctionType
+
+P = 128
+PACK = 4
+B, N, HID, D = 128, 32, 512, 256
+D_HALVES = D // P
+LN_EPS = 1e-5
+FMIN, FMAX, TICK_INTERVAL = 0.5, 40.0, 0.1
+PI = 3.141592653589793
+SINE_TERMS = 16
+
+GROUP = 4
+RUN = 4
+W2_SCALAR_WORDS = 96
+
+FLOPS = 2 * B * N * HID * (HID + D)
+
+
+def sine(angle):
+    x = (angle + PI) % (2.0 * PI) - PI
+    term, total = x, x
+    for k in range(1, SINE_TERMS):
+        term = -term * x * x / ((2 * k) * (2 * k + 1))
+        total = total + term
+    return total
+
+
+def oscillator_gain(n, tick):
+    freq = FMIN * (FMAX / FMIN) ** (n / (N - 1))
+    phase = (n * 2.3571) % (2.0 * PI)
+    return 1.0 + 0.5 * sine(2.0 * PI * freq * tick * TICK_INTERVAL + phase)
+
+
+def rows_in_runs(rows):
+    return rows.rearrange("p t (c i) -> p c t i", i=RUN)
+
+
+def words_in_runs(grouped):
+    return grouped.rearrange("p (c i) t -> p c t i", i=RUN)
+
+
+def tile_neuronpool_pa_kernel(tc, h1, W2, b2, W3, b3, gamma, beta, tick, out):
+    nc = tc.nc
+    with ExitStack() as stack:
+        consts = stack.enter_context(tc.tile_pool(name="consts", bufs=1))
+        loads = stack.enter_context(tc.tile_pool(name="loads", bufs=8))
+        work = stack.enter_context(tc.tile_pool(name="work", bufs=3))
+        stats = stack.enter_context(tc.tile_pool(name="stats", bufs=4))
+        psum_pairs = stack.enter_context(tc.psum_pool(name="psum_pairs", bufs=2))
+        psum_single = stack.enter_context(tc.psum_pool(name="psum_single", bufs=1))
+
+        identity = consts.tile([P, P], F32)
+        make_identity(nc, identity[:])
+        minus_half = consts.tile([P, 1], F32)
+        nc.vector.memset(minus_half[:], -0.5)
+
+        b2_rows = consts.tile([P, HID], BF16)
+        nc.vector.memset(b2_rows[:], 0.0)
+        nc.sync.dma_start(out=b2_rows[0:N, :], in_=b2)
+        b2_sorted = consts.tile([P, PACK, P], F32)
+        nc.vector.tensor_copy(
+            out=b2_sorted[:], in_=b2_rows[:].rearrange("n (p t) -> n t p", t=PACK)
+        )
+        b2_turned = psum_pairs.tile([P, PACK, P], F32, tag="hidden")
+        for t in range(PACK):
+            nc.tensor.transpose(out=b2_turned[:, t, :], in_=b2_sorted[:, t, :], identity=identity[:])
+        b2_cols = consts.tile([P, PACK, N], F32)
+        nc.vector.tensor_copy(out=b2_cols[:], in_=b2_turned[:, :, 0:N])
+
+        ln_rows = consts.tile([P, D], BF16)
+        nc.vector.memset(ln_rows[:], 0.0)
+        for k, vector in enumerate((b3, gamma, beta)):
+            nc.sync.dma_start(out=ln_rows[k * N : (k + 1) * N, :], in_=vector)
+        ln_rows_f32 = consts.tile([P, D], F32)
+        nc.vector.tensor_copy(out=ln_rows_f32[:], in_=ln_rows[:])
+        ln_turned = psum_single.tile([P, D_HALVES, P], F32, tag="x_turned")
+        for h in range(D_HALVES):
+            nc.tensor.transpose(
+                out=ln_turned[:, h, :], in_=ln_rows_f32[:, h * P : (h + 1) * P], identity=identity[:]
+            )
+        ln_cols = consts.tile([P, D_HALVES, P], F32)
+        nc.vector.tensor_copy(out=ln_cols[:], in_=ln_turned[:])
+        beta_gain_cols = consts.tile([P, D_HALVES, N], F32)
+
+        def spread(dst, cols, column):
+            for h in range(D_HALVES):
+                nc.tensor.transpose(
+                    out=dst[:, h * P : (h + 1) * P],
+                    in_=cols[:, h, column : column + 1].to_broadcast([P, P]),
+                    identity=identity[:],
+                )
+
+        for first in range(0, N, GROUP):
+            x_rows = loads.tile([P, GROUP, HID], BF16, bufs=3)
+            nc.sync.dma_start(out=x_rows[:], in_=h1[:, first : first + GROUP, :])
+            results = work.tile([P, GROUP, D], F32)
+
+            for i in range(GROUP):
+                n = first + i
+                gain = oscillator_gain(n, tick)
+
+                w2_rows = loads.tile([P, PACK, HID], BF16)
+                nc.sync.dma_start(out=w2_rows[:], in_=W2[n].rearrange("(p t) j -> p t j", t=PACK))
+                w3_rows = loads.tile([P, PACK, D], BF16)
+                nc.sync.dma_start(out=w3_rows[:], in_=W3[n].rearrange("(p t) d -> p t d", t=PACK))
+
+                x_words = x_rows[:, i, :].bitcast(F32).rearrange("b (p u) -> b u p", u=2)
+                x_turned = psum_single.tile([P, 2, B], F32)
+                for u in range(2):
+                    nc.tensor.transpose(out=x_turned[:, u, :], in_=x_words[:, u, :], identity=identity[:])
+                x_grouped = work.tile([P, B, PACK], BF16, align_bytes=64)
+                nc.scalar.copy(
+                    out=x_grouped[:].rearrange("p b t -> p (b t)").bitcast(F32).rearrange(
+                        "p (b u) -> p b u", u=2
+                    ),
+                    in_=x_turned[:].rearrange("p u b -> p b u"),
+                )
+                x_codes = work.tile([P, B], U32, align_bytes=64)
+                x_scales = work.tile([P, B], U8, align_bytes=64)
+                nc.vector.quantize_mx(
+                    out=x_codes[:].bitcast(FP8X4),
+                    scales=x_scales[:],
+                    in_=x_grouped[:].rearrange("p b t -> p (b t)"),
+                )
+
+                w2_grouped = work.tile([P, PACK, P, PACK], BF16, align_bytes=64)
+                w2_src = rows_in_runs(w2_rows[:])
+                w2_dst = w2_grouped[:].rearrange("p i c t -> p c t i")
+                nc.scalar.copy(out=w2_dst[:, :W2_SCALAR_WORDS], in_=w2_src[:, :W2_SCALAR_WORDS])
+                nc.vector.tensor_copy(out=w2_dst[:, W2_SCALAR_WORDS:], in_=w2_src[:, W2_SCALAR_WORDS:])
+                w2_codes = work.tile([P, HID], U32, align_bytes=64)
+                w2_scales = work.tile([P, HID], U8, align_bytes=64)
+                nc.vector.quantize_mx(
+                    out=w2_codes[:].bitcast(FP8X4),
+                    scales=w2_scales[:],
+                    in_=w2_grouped[:].rearrange("p i c t -> p (i c t)"),
+                )
+
+                w3_grouped = work.tile([P, D, PACK], BF16, align_bytes=64)
+                nc.vector.tensor_copy(out=words_in_runs(w3_grouped[:]), in_=rows_in_runs(w3_rows[:]))
+                w3_codes = work.tile([P, D], U32, align_bytes=64)
+                w3_scales = work.tile([P, D], U8, align_bytes=64)
+                nc.vector.quantize_mx(
+                    out=w3_codes[:].bitcast(FP8X4),
+                    scales=w3_scales[:],
+                    in_=w3_grouped[:].rearrange("p d t -> p (d t)"),
+                )
+
+                hidden = psum_pairs.tile([P, PACK, B], F32)
+                for t in range(PACK):
+                    nc.tensor.matmul_mx(
+                        out=hidden[:, t, :],
+                        lhsT=w2_codes[:, t * P : (t + 1) * P].bitcast(FP8X4),
+                        lhsT_scale=w2_scales[:, t * P : (t + 1) * P],
+                        rhs=x_codes[:].bitcast(FP8X4),
+                        rhs_scale=x_scales[:],
+                        start=True,
+                        stop=True,
+                    )
+                g_rows = work.tile([P, PACK, B], BF16)
+                for t in range(PACK):
+                    nc.scalar.activation(
+                        out=g_rows[:, t, :],
+                        in_=hidden[:, t, :],
+                        func=ACT.Gelu,
+                        bias=b2_cols[:, t, n : n + 1],
+                        scale=1.0,
+                    )
+                g_grouped = work.tile([P, B, PACK], BF16, align_bytes=64)
+                nc.vector.tensor_copy(out=words_in_runs(g_grouped[:]), in_=rows_in_runs(g_rows[:]))
+                g_codes = work.tile([P, B], U32, align_bytes=64)
+                g_scales = work.tile([P, B], U8, align_bytes=64)
+                nc.vector.quantize_mx(
+                    out=g_codes[:].bitcast(FP8X4),
+                    scales=g_scales[:],
+                    in_=g_grouped[:].rearrange("p b t -> p (b t)"),
+                )
+
+                nc.gpsimd.tensor_scalar(
+                    out=beta_gain_cols[:, :, n : n + 1],
+                    in0=ln_cols[:, :, 2 * N + n : 2 * N + n + 1],
+                    scalar1=gain,
+                    scalar2=0.0,
+                    op0=ALU.mult,
+                    op1=ALU.add,
+                )
+                b3_spread = psum_single.tile([P, D], F32)
+                spread(b3_spread, ln_cols, n)
+                affine_spread = psum_pairs.tile([P, 2, D], F32)
+                spread(affine_spread[:, 0, :], ln_cols, N + n)
+                spread(affine_spread[:, 1, :], beta_gain_cols, n)
+                b3_all = work.tile([P, D], F32)
+                nc.scalar.copy(out=b3_all[:], in_=b3_spread[:])
+
+                y_sums = psum_pairs.tile([P, D], F32)
+                nc.tensor.matmul_mx(
+                    out=y_sums[:],
+                    lhsT=g_codes[:].bitcast(FP8X4),
+                    lhsT_scale=g_scales[:],
+                    rhs=w3_codes[:].bitcast(FP8X4),
+                    rhs_scale=w3_scales[:],
+                    start=True,
+                    stop=True,
+                )
+                y = work.tile([P, D], F32)
+                y_total = stats.tile([P, 1], F32)
+                nc.vector.scalar_tensor_tensor(
+                    out=y[:], in0=y_sums[:], scalar=1.0, in1=b3_all[:],
+                    op0=ALU.mult, op1=ALU.add, accum_out=y_total[:],
+                )
+                mean = stats.tile([P, 1], F32)
+                nc.vector.tensor_scalar_mul(out=mean[:], in0=y_total[:], scalar1=1.0 / D)
+                squares = work.tile([P, D], F32)
+                square_total = stats.tile([P, 1], F32)
+                nc.scalar.activation(
+                    out=squares[:], in_=y[:], func=ACT.Square, bias=mean[:], scale=-1.0,
+                    accum_out=square_total[:],
+                )
+                spread_sq = stats.tile([P, 1], F32)
+                nc.gpsimd.tensor_scalar(
+                    out=spread_sq[:], in0=square_total[:],
+                    scalar1=1.0 / (D * gain * gain), scalar2=LN_EPS / (gain * gain),
+                    op0=ALU.mult, op1=ALU.add,
+                )
+                rstd_gain = stats.tile([P, 1], F32)
+                nc.gpsimd.tensor_tensor(out=rstd_gain[:], in0=spread_sq[:], in1=minus_half[:], op=ALU.pow)
+                centred = work.tile([P, D], F32)
+                nc.vector.scalar_tensor_tensor(
+                    out=centred[:], in0=y[:], scalar=mean[:], in1=affine_spread[:, 0, :],
+                    op0=ALU.subtract, op1=ALU.mult,
+                )
+                nc.vector.scalar_tensor_tensor(
+                    out=results[:, i, :], in0=centred[:], scalar=rstd_gain[:], in1=affine_spread[:, 1, :],
+                    op0=ALU.mult, op1=ALU.add,
+                )
+
+            nc.sync.dma_start(out=out[:, first : first + GROUP, :], in_=results[:])

@@ -22,7 +22,7 @@ SINE_TERMS = 16
 
 GROUP = 4
 RUN = 4
-W2_SCALAR_WORDS = 96
+W2_SCALAR_RUNS = 96
 
 FLOPS = 2 * B * N * HID * (HID + D)
 
@@ -68,13 +68,11 @@ def tile_neuronpool_pa_kernel(tc, h1, W2, b2, W3, b3, gamma, beta, tick, out):
         b2_rows = consts.tile([P, HID], BF16)
         nc.vector.memset(b2_rows[:], 0.0)
         nc.sync.dma_start(out=b2_rows[0:N, :], in_=b2)
-        b2_sorted = consts.tile([P, PACK, P], F32)
-        nc.vector.tensor_copy(
-            out=b2_sorted[:], in_=b2_rows[:].rearrange("n (p t) -> n t p", t=PACK)
-        )
+        b2_rows_f32 = consts.tile([P, PACK, P], F32)
+        nc.vector.tensor_copy(out=b2_rows_f32[:], in_=b2_rows[:].rearrange("n (t p) -> n t p", p=P))
         b2_turned = psum_pairs.tile([P, PACK, P], F32, tag="hidden")
         for t in range(PACK):
-            nc.tensor.transpose(out=b2_turned[:, t, :], in_=b2_sorted[:, t, :], identity=identity[:])
+            nc.tensor.transpose(out=b2_turned[:, t, :], in_=b2_rows_f32[:, t, :], identity=identity[:])
         b2_cols = consts.tile([P, PACK, N], F32)
         nc.vector.tensor_copy(out=b2_cols[:], in_=b2_turned[:, :, 0:N])
 
@@ -113,7 +111,7 @@ def tile_neuronpool_pa_kernel(tc, h1, W2, b2, W3, b3, gamma, beta, tick, out):
                 w2_rows = loads.tile([P, PACK, HID], BF16)
                 nc.sync.dma_start(out=w2_rows[:], in_=W2[n].rearrange("(p t) j -> p t j", t=PACK))
                 w3_rows = loads.tile([P, PACK, D], BF16)
-                nc.sync.dma_start(out=w3_rows[:], in_=W3[n].rearrange("(p t) d -> p t d", t=PACK))
+                nc.sync.dma_start(out=w3_rows[:], in_=W3[n].rearrange("(t p) d -> p t d", p=P))
 
                 x_words = x_rows[:, i, :].bitcast(F32).rearrange("b (p u) -> b u p", u=2)
                 x_turned = psum_single.tile([P, 2, B], F32)
@@ -134,17 +132,17 @@ def tile_neuronpool_pa_kernel(tc, h1, W2, b2, W3, b3, gamma, beta, tick, out):
                     in_=x_grouped[:].rearrange("p b t -> p (b t)"),
                 )
 
-                w2_grouped = work.tile([P, PACK, P, PACK], BF16, align_bytes=64)
+                w2_grouped = work.tile([P, HID, PACK], BF16, align_bytes=64)
                 w2_src = rows_in_runs(w2_rows[:])
-                w2_dst = w2_grouped[:].rearrange("p i c t -> p c t i")
-                nc.scalar.copy(out=w2_dst[:, :W2_SCALAR_WORDS], in_=w2_src[:, :W2_SCALAR_WORDS])
-                nc.vector.tensor_copy(out=w2_dst[:, W2_SCALAR_WORDS:], in_=w2_src[:, W2_SCALAR_WORDS:])
+                w2_dst = words_in_runs(w2_grouped[:])
+                nc.scalar.copy(out=w2_dst[:, :W2_SCALAR_RUNS], in_=w2_src[:, :W2_SCALAR_RUNS])
+                nc.vector.tensor_copy(out=w2_dst[:, W2_SCALAR_RUNS:], in_=w2_src[:, W2_SCALAR_RUNS:])
                 w2_codes = work.tile([P, HID], U32, align_bytes=64)
                 w2_scales = work.tile([P, HID], U8, align_bytes=64)
                 nc.vector.quantize_mx(
                     out=w2_codes[:].bitcast(FP8X4),
                     scales=w2_scales[:],
-                    in_=w2_grouped[:].rearrange("p i c t -> p (i c t)"),
+                    in_=w2_grouped[:].rearrange("p j t -> p (j t)"),
                 )
 
                 w3_grouped = work.tile([P, D, PACK], BF16, align_bytes=64)

@@ -22,7 +22,10 @@ SINE_TERMS = 16
 
 GROUP = 4
 RUN = 4
-W2_SCALAR_RUNS = 96
+W2_SCALAR_WORDS = 96
+FIRST_STEP, LAST_STEP = -2, N + 3
+LOADS_AHEAD = 4
+LOAD_BUFS = LOADS_AHEAD + 3
 
 FLOPS = 2 * B * N * HID * (HID + D)
 
@@ -54,11 +57,21 @@ def tile_neuronpool_pa_kernel(tc, h1, W2, b2, W3, b3, gamma, beta, tick, out):
     nc = tc.nc
     with ExitStack() as stack:
         consts = stack.enter_context(tc.tile_pool(name="consts", bufs=1))
-        loads = stack.enter_context(tc.tile_pool(name="loads", bufs=8))
-        work = stack.enter_context(tc.tile_pool(name="work", bufs=3))
-        stats = stack.enter_context(tc.tile_pool(name="stats", bufs=4))
+        loads = stack.enter_context(tc.tile_pool(name="loads", bufs=LOAD_BUFS))
+        work = stack.enter_context(tc.tile_pool(name="work", bufs=4))
         psum_pairs = stack.enter_context(tc.psum_pool(name="psum_pairs", bufs=2))
         psum_single = stack.enter_context(tc.psum_pool(name="psum_single", bufs=1))
+        stack.enter_context(tc.manual_schedule())
+
+        tiles = {}
+
+        def make(pool, name, n, shape, dtype):
+            tiles[name, n] = pool.tile(shape, dtype, name=name, align_bytes=64)
+            return tiles[name, n]
+
+        def make_bank(pool, name, n, shape):
+            tiles[name, n] = pool.tile(shape, F32, name=name)
+            return tiles[name, n]
 
         identity = consts.tile([P, P], F32)
         make_identity(nc, identity[:])
@@ -68,18 +81,31 @@ def tile_neuronpool_pa_kernel(tc, h1, W2, b2, W3, b3, gamma, beta, tick, out):
         b2_rows = consts.tile([P, HID], BF16)
         nc.vector.memset(b2_rows[:], 0.0)
         nc.sync.dma_start(out=b2_rows[0:N, :], in_=b2)
-        b2_rows_f32 = consts.tile([P, PACK, P], F32)
-        nc.vector.tensor_copy(out=b2_rows_f32[:], in_=b2_rows[:].rearrange("n (t p) -> n t p", p=P))
+        ln_rows = consts.tile([P, D], BF16)
+        nc.vector.memset(ln_rows[:], 0.0)
+        for v, vector in enumerate((b3, gamma, beta)):
+            nc.sync.dma_start(out=ln_rows[v * N : (v + 1) * N, :], in_=vector)
+
+        def load(n):
+            if n % GROUP == 0:
+                x_rows = make(loads, "x_rows", n // GROUP, [P, GROUP, HID], BF16)
+                nc.sync.dma_start(out=x_rows[:], in_=h1[:, n : n + GROUP, :])
+            w2_rows = make(loads, "w2_rows", n, [P, PACK, HID], BF16)
+            nc.sync.dma_start(out=w2_rows[:], in_=W2[n].rearrange("(p t) j -> p t j", t=PACK))
+            w3_rows = make(loads, "w3_rows", n, [P, PACK, D], BF16)
+            nc.sync.dma_start(out=w3_rows[:], in_=W3[n].rearrange("(p t) d -> p t d", t=PACK))
+
+        for n in range(LOADS_AHEAD):
+            load(n)
+
+        b2_sorted = consts.tile([P, PACK, P], F32)
+        nc.vector.tensor_copy(out=b2_sorted[:], in_=b2_rows[:].rearrange("n (p t) -> n t p", t=PACK))
         b2_turned = psum_pairs.tile([P, PACK, P], F32, tag="hidden")
         for t in range(PACK):
-            nc.tensor.transpose(out=b2_turned[:, t, :], in_=b2_rows_f32[:, t, :], identity=identity[:])
+            nc.tensor.transpose(out=b2_turned[:, t, :], in_=b2_sorted[:, t, :], identity=identity[:])
         b2_cols = consts.tile([P, PACK, N], F32)
         nc.vector.tensor_copy(out=b2_cols[:], in_=b2_turned[:, :, 0:N])
 
-        ln_rows = consts.tile([P, D], BF16)
-        nc.vector.memset(ln_rows[:], 0.0)
-        for k, vector in enumerate((b3, gamma, beta)):
-            nc.sync.dma_start(out=ln_rows[k * N : (k + 1) * N, :], in_=vector)
         ln_rows_f32 = consts.tile([P, D], F32)
         nc.vector.tensor_copy(out=ln_rows_f32[:], in_=ln_rows[:])
         ln_turned = psum_single.tile([P, D_HALVES, P], F32, tag="x_turned")
@@ -99,148 +125,214 @@ def tile_neuronpool_pa_kernel(tc, h1, W2, b2, W3, b3, gamma, beta, tick, out):
                     identity=identity[:],
                 )
 
-        for first in range(0, N, GROUP):
-            x_rows = loads.tile([P, GROUP, HID], BF16, bufs=3)
-            nc.sync.dma_start(out=x_rows[:], in_=h1[:, first : first + GROUP, :])
-            results = work.tile([P, GROUP, D], F32)
+        def quantise(name, n, grouped, width):
+            codes = make(work, name + "_codes", n, [P, width], U32)
+            scales = make(work, name + "_scales", n, [P, width], U8)
+            nc.vector.quantize_mx(out=codes[:].bitcast(FP8X4), scales=scales[:], in_=grouped)
 
-            for i in range(GROUP):
-                n = first + i
-                gain = oscillator_gain(n, tick)
+        def turn_x(n):
+            x_rows = tiles["x_rows", n // GROUP]
+            x_words = x_rows[:, n % GROUP, :].bitcast(F32).rearrange("b (p u) -> b u p", u=2)
+            x_turned = make_bank(psum_single, "x_turned", n, [P, 2, B])
+            for u in range(2):
+                nc.tensor.transpose(out=x_turned[:, u, :], in_=x_words[:, u, :], identity=identity[:])
 
-                w2_rows = loads.tile([P, PACK, HID], BF16)
-                nc.sync.dma_start(out=w2_rows[:], in_=W2[n].rearrange("(p t) j -> p t j", t=PACK))
-                w3_rows = loads.tile([P, PACK, D], BF16)
-                nc.sync.dma_start(out=w3_rows[:], in_=W3[n].rearrange("(t p) d -> p t d", p=P))
+        def copy_x(n):
+            x_grouped = make(work, "x_grouped", n, [P, B, PACK], BF16)
+            nc.scalar.copy(
+                out=x_grouped[:].rearrange("p b t -> p (b t)").bitcast(F32).rearrange(
+                    "p (b u) -> p b u", u=2
+                ),
+                in_=tiles["x_turned", n][:].rearrange("p u b -> p b u"),
+            )
 
-                x_words = x_rows[:, i, :].bitcast(F32).rearrange("b (p u) -> b u p", u=2)
-                x_turned = psum_single.tile([P, 2, B], F32)
-                for u in range(2):
-                    nc.tensor.transpose(out=x_turned[:, u, :], in_=x_words[:, u, :], identity=identity[:])
-                x_grouped = work.tile([P, B, PACK], BF16, align_bytes=64)
-                nc.scalar.copy(
-                    out=x_grouped[:].rearrange("p b t -> p (b t)").bitcast(F32).rearrange(
-                        "p (b u) -> p b u", u=2
-                    ),
-                    in_=x_turned[:].rearrange("p u b -> p b u"),
-                )
-                x_codes = work.tile([P, B], U32, align_bytes=64)
-                x_scales = work.tile([P, B], U8, align_bytes=64)
-                nc.vector.quantize_mx(
-                    out=x_codes[:].bitcast(FP8X4),
-                    scales=x_scales[:],
-                    in_=x_grouped[:].rearrange("p b t -> p (b t)"),
-                )
+        def quantise_x(n):
+            quantise("x", n, tiles["x_grouped", n][:].rearrange("p b t -> p (b t)"), B)
 
-                w2_grouped = work.tile([P, HID, PACK], BF16, align_bytes=64)
-                w2_src = rows_in_runs(w2_rows[:])
-                w2_dst = words_in_runs(w2_grouped[:])
-                nc.scalar.copy(out=w2_dst[:, :W2_SCALAR_RUNS], in_=w2_src[:, :W2_SCALAR_RUNS])
-                nc.vector.tensor_copy(out=w2_dst[:, W2_SCALAR_RUNS:], in_=w2_src[:, W2_SCALAR_RUNS:])
-                w2_codes = work.tile([P, HID], U32, align_bytes=64)
-                w2_scales = work.tile([P, HID], U8, align_bytes=64)
-                nc.vector.quantize_mx(
-                    out=w2_codes[:].bitcast(FP8X4),
-                    scales=w2_scales[:],
-                    in_=w2_grouped[:].rearrange("p j t -> p (j t)"),
-                )
+        def regroup_w2_on_scalar(n):
+            w2_grouped = make(work, "w2_grouped", n, [P, PACK, P, PACK], BF16)
+            nc.scalar.copy(
+                out=w2_grouped[:].rearrange("p i c t -> p c t i")[:, :W2_SCALAR_WORDS],
+                in_=rows_in_runs(tiles["w2_rows", n][:])[:, :W2_SCALAR_WORDS],
+            )
 
-                w3_grouped = work.tile([P, D, PACK], BF16, align_bytes=64)
-                nc.vector.tensor_copy(out=words_in_runs(w3_grouped[:]), in_=rows_in_runs(w3_rows[:]))
-                w3_codes = work.tile([P, D], U32, align_bytes=64)
-                w3_scales = work.tile([P, D], U8, align_bytes=64)
-                nc.vector.quantize_mx(
-                    out=w3_codes[:].bitcast(FP8X4),
-                    scales=w3_scales[:],
-                    in_=w3_grouped[:].rearrange("p d t -> p (d t)"),
-                )
+        def regroup_w2_on_vector(n):
+            nc.vector.tensor_copy(
+                out=tiles["w2_grouped", n][:].rearrange("p i c t -> p c t i")[:, W2_SCALAR_WORDS:],
+                in_=rows_in_runs(tiles["w2_rows", n][:])[:, W2_SCALAR_WORDS:],
+            )
 
-                hidden = psum_pairs.tile([P, PACK, B], F32)
-                for t in range(PACK):
-                    nc.tensor.matmul_mx(
-                        out=hidden[:, t, :],
-                        lhsT=w2_codes[:, t * P : (t + 1) * P].bitcast(FP8X4),
-                        lhsT_scale=w2_scales[:, t * P : (t + 1) * P],
-                        rhs=x_codes[:].bitcast(FP8X4),
-                        rhs_scale=x_scales[:],
-                        start=True,
-                        stop=True,
-                    )
-                g_rows = work.tile([P, PACK, B], BF16)
-                for t in range(PACK):
-                    nc.scalar.activation(
-                        out=g_rows[:, t, :],
-                        in_=hidden[:, t, :],
-                        func=ACT.Gelu,
-                        bias=b2_cols[:, t, n : n + 1],
-                        scale=1.0,
-                    )
-                g_grouped = work.tile([P, B, PACK], BF16, align_bytes=64)
-                nc.vector.tensor_copy(out=words_in_runs(g_grouped[:]), in_=rows_in_runs(g_rows[:]))
-                g_codes = work.tile([P, B], U32, align_bytes=64)
-                g_scales = work.tile([P, B], U8, align_bytes=64)
-                nc.vector.quantize_mx(
-                    out=g_codes[:].bitcast(FP8X4),
-                    scales=g_scales[:],
-                    in_=g_grouped[:].rearrange("p b t -> p (b t)"),
-                )
+        def quantise_w2(n):
+            quantise("w2", n, tiles["w2_grouped", n][:].rearrange("p i c t -> p (i c t)"), HID)
 
-                nc.gpsimd.tensor_scalar(
-                    out=beta_gain_cols[:, :, n : n + 1],
-                    in0=ln_cols[:, :, 2 * N + n : 2 * N + n + 1],
-                    scalar1=gain,
-                    scalar2=0.0,
-                    op0=ALU.mult,
-                    op1=ALU.add,
-                )
-                b3_spread = psum_single.tile([P, D], F32)
-                spread(b3_spread, ln_cols, n)
-                affine_spread = psum_pairs.tile([P, 2, D], F32)
-                spread(affine_spread[:, 0, :], ln_cols, N + n)
-                spread(affine_spread[:, 1, :], beta_gain_cols, n)
-                b3_all = work.tile([P, D], F32)
-                nc.scalar.copy(out=b3_all[:], in_=b3_spread[:])
+        def regroup_w3(n):
+            w3_grouped = make(work, "w3_grouped", n, [P, D, PACK], BF16)
+            nc.vector.tensor_copy(
+                out=words_in_runs(w3_grouped[:]), in_=rows_in_runs(tiles["w3_rows", n][:])
+            )
 
-                y_sums = psum_pairs.tile([P, D], F32)
+        def quantise_w3(n):
+            quantise("w3", n, tiles["w3_grouped", n][:].rearrange("p d t -> p (d t)"), D)
+
+        def first_layer(n):
+            hidden = make_bank(psum_pairs, "hidden", n, [P, PACK, B])
+            for t in range(PACK):
                 nc.tensor.matmul_mx(
-                    out=y_sums[:],
-                    lhsT=g_codes[:].bitcast(FP8X4),
-                    lhsT_scale=g_scales[:],
-                    rhs=w3_codes[:].bitcast(FP8X4),
-                    rhs_scale=w3_scales[:],
+                    out=hidden[:, t, :],
+                    lhsT=tiles["w2_codes", n][:, t * P : (t + 1) * P].bitcast(FP8X4),
+                    lhsT_scale=tiles["w2_scales", n][:, t * P : (t + 1) * P],
+                    rhs=tiles["x_codes", n][:].bitcast(FP8X4),
+                    rhs_scale=tiles["x_scales", n][:],
                     start=True,
                     stop=True,
                 )
-                y = work.tile([P, D], F32)
-                y_total = stats.tile([P, 1], F32)
-                nc.vector.scalar_tensor_tensor(
-                    out=y[:], in0=y_sums[:], scalar=1.0, in1=b3_all[:],
-                    op0=ALU.mult, op1=ALU.add, accum_out=y_total[:],
-                )
-                mean = stats.tile([P, 1], F32)
-                nc.vector.tensor_scalar_mul(out=mean[:], in0=y_total[:], scalar1=1.0 / D)
-                squares = work.tile([P, D], F32)
-                square_total = stats.tile([P, 1], F32)
+
+        def gelu(n):
+            g_rows = make(work, "g_rows", n, [P, PACK, B], BF16)
+            for t in range(PACK):
                 nc.scalar.activation(
-                    out=squares[:], in_=y[:], func=ACT.Square, bias=mean[:], scale=-1.0,
-                    accum_out=square_total[:],
-                )
-                spread_sq = stats.tile([P, 1], F32)
-                nc.gpsimd.tensor_scalar(
-                    out=spread_sq[:], in0=square_total[:],
-                    scalar1=1.0 / (D * gain * gain), scalar2=LN_EPS / (gain * gain),
-                    op0=ALU.mult, op1=ALU.add,
-                )
-                rstd_gain = stats.tile([P, 1], F32)
-                nc.gpsimd.tensor_tensor(out=rstd_gain[:], in0=spread_sq[:], in1=minus_half[:], op=ALU.pow)
-                centred = work.tile([P, D], F32)
-                nc.vector.scalar_tensor_tensor(
-                    out=centred[:], in0=y[:], scalar=mean[:], in1=affine_spread[:, 0, :],
-                    op0=ALU.subtract, op1=ALU.mult,
-                )
-                nc.vector.scalar_tensor_tensor(
-                    out=results[:, i, :], in0=centred[:], scalar=rstd_gain[:], in1=affine_spread[:, 1, :],
-                    op0=ALU.mult, op1=ALU.add,
+                    out=g_rows[:, t, :],
+                    in_=tiles["hidden", n][:, t, :],
+                    func=ACT.Gelu,
+                    bias=b2_cols[:, t, n : n + 1],
+                    scale=1.0,
                 )
 
-            nc.sync.dma_start(out=out[:, first : first + GROUP, :], in_=results[:])
+        def regroup_g(n):
+            g_grouped = make(work, "g_grouped", n, [P, B, PACK], BF16)
+            nc.vector.tensor_copy(
+                out=words_in_runs(g_grouped[:]), in_=rows_in_runs(tiles["g_rows", n][:])
+            )
+
+        def quantise_g(n):
+            quantise("g", n, tiles["g_grouped", n][:].rearrange("p b t -> p (b t)"), B)
+
+        def second_layer(n):
+            y_sums = make_bank(psum_pairs, "y_sums", n, [P, D])
+            nc.tensor.matmul_mx(
+                out=y_sums[:],
+                lhsT=tiles["g_codes", n][:].bitcast(FP8X4),
+                lhsT_scale=tiles["g_scales", n][:],
+                rhs=tiles["w3_codes", n][:].bitcast(FP8X4),
+                rhs_scale=tiles["w3_scales", n][:],
+                start=True,
+                stop=True,
+            )
+
+        def spread_b3(n):
+            spread(make_bank(psum_single, "b3_spread", n, [P, D]), ln_cols, n)
+
+        def copy_b3(n):
+            nc.scalar.copy(out=make(work, "b3_all", n, [P, D], F32)[:], in_=tiles["b3_spread", n][:])
+
+        def spread_gamma(n):
+            spread(make_bank(psum_single, "gamma_spread", n, [P, D]), ln_cols, N + n)
+
+        def scale_beta(n):
+            nc.scalar.mul(
+                out=beta_gain_cols[:, :, n : n + 1],
+                in_=ln_cols[:, :, 2 * N + n : 2 * N + n + 1],
+                mul=oscillator_gain(n, tick),
+            )
+
+        def spread_beta(n):
+            spread(make_bank(psum_single, "beta_spread", n, [P, D]), beta_gain_cols, n)
+
+        def add_b3(n):
+            nc.vector.scalar_tensor_tensor(
+                out=make(work, "y", n, [P, D], F32)[:],
+                in0=tiles["y_sums", n][:],
+                scalar=1.0,
+                in1=tiles["b3_all", n][:],
+                op0=ALU.mult,
+                op1=ALU.add,
+                accum_out=make(work, "y_total", n, [P, 1], F32)[:],
+            )
+
+        def take_mean(n):
+            nc.vector.tensor_scalar_mul(
+                out=make(work, "mean", n, [P, 1], F32)[:], in0=tiles["y_total", n][:], scalar1=1.0 / D
+            )
+
+        def sum_squares(n):
+            nc.scalar.activation(
+                out=make(work, "squares", n, [P, D], F32)[:],
+                in_=tiles["y", n][:],
+                func=ACT.Square,
+                bias=tiles["mean", n][:],
+                scale=-1.0,
+                accum_out=make(work, "square_total", n, [P, 1], F32)[:],
+            )
+
+        def take_rstd(n):
+            gain = oscillator_gain(n, tick)
+            nc.gpsimd.tensor_scalar(
+                out=make(work, "scaled_var", n, [P, 1], F32)[:],
+                in0=tiles["square_total", n][:],
+                scalar1=1.0 / (D * gain * gain),
+                scalar2=LN_EPS / (gain * gain),
+                op0=ALU.mult,
+                op1=ALU.add,
+            )
+            nc.gpsimd.tensor_tensor(
+                out=make(work, "rstd_gain", n, [P, 1], F32)[:],
+                in0=tiles["scaled_var", n][:],
+                in1=minus_half[:],
+                op=ALU.pow,
+            )
+
+        def centre(n):
+            nc.vector.scalar_tensor_tensor(
+                out=make(work, "centred", n, [P, D], F32)[:],
+                in0=tiles["y", n][:],
+                scalar=tiles["mean", n][:],
+                in1=tiles["gamma_spread", n][:],
+                op0=ALU.subtract,
+                op1=ALU.mult,
+            )
+
+        def finish(n):
+            if n % GROUP == 0:
+                make(work, "results", n // GROUP, [P, GROUP, D], F32)
+            results = tiles["results", n // GROUP]
+            nc.vector.scalar_tensor_tensor(
+                out=results[:, n % GROUP, :],
+                in0=tiles["centred", n][:],
+                scalar=tiles["rstd_gain", n][:],
+                in1=tiles["beta_spread", n][:],
+                op0=ALU.mult,
+                op1=ALU.add,
+            )
+            if n % GROUP == GROUP - 1:
+                nc.sync.dma_start(out=out[:, n - GROUP + 1 : n + 1, :], in_=results[:])
+
+        def run(stage, n):
+            if 0 <= n < N:
+                stage(n)
+
+        for k in range(FIRST_STEP, LAST_STEP + 1):
+            run(load, k - FIRST_STEP + LOADS_AHEAD)
+            run(first_layer, k - 1)
+            run(regroup_w2_on_scalar, k)
+            run(scale_beta, k)
+            run(regroup_w3, k)
+            run(add_b3, k - 3)
+            run(spread_beta, k - 4)
+            run(spread_b3, k - 2)
+            run(regroup_w2_on_vector, k)
+            run(take_mean, k - 3)
+            run(copy_x, k + 1)
+            run(regroup_g, k - 2)
+            run(centre, k - 3)
+            run(sum_squares, k - 3)
+            run(take_rstd, k - 3)
+            run(spread_gamma, k - 2)
+            run(turn_x, k + 2)
+            run(quantise_w3, k)
+            run(quantise_x, k)
+            run(gelu, k - 1)
+            run(finish, k - 4)
+            run(quantise_g, k - 2)
+            run(second_layer, k - 2)
+            run(copy_b3, k - 2)
+            run(quantise_w2, k)

@@ -22,7 +22,7 @@ SINE_TERMS = 16
 
 GROUP = 4
 RUN = 4
-W2_SCALAR_WORDS = 96
+W2_SCALAR_RUNS = 96
 FIRST_STEP, LAST_STEP = -2, N + 3
 LOADS_AHEAD = 4
 LOAD_BUFS = LOADS_AHEAD + 3
@@ -93,16 +93,16 @@ def tile_neuronpool_pa_kernel(tc, h1, W2, b2, W3, b3, gamma, beta, tick, out):
             w2_rows = make(loads, "w2_rows", n, [P, PACK, HID], BF16)
             nc.sync.dma_start(out=w2_rows[:], in_=W2[n].rearrange("(p t) j -> p t j", t=PACK))
             w3_rows = make(loads, "w3_rows", n, [P, PACK, D], BF16)
-            nc.sync.dma_start(out=w3_rows[:], in_=W3[n].rearrange("(p t) d -> p t d", t=PACK))
+            nc.sync.dma_start(out=w3_rows[:], in_=W3[n].rearrange("(t p) d -> p t d", p=P))
 
         for n in range(LOADS_AHEAD):
             load(n)
 
-        b2_sorted = consts.tile([P, PACK, P], F32)
-        nc.vector.tensor_copy(out=b2_sorted[:], in_=b2_rows[:].rearrange("n (p t) -> n t p", t=PACK))
+        b2_rows_f32 = consts.tile([P, PACK, P], F32)
+        nc.vector.tensor_copy(out=b2_rows_f32[:], in_=b2_rows[:].rearrange("n (t p) -> n t p", p=P))
         b2_turned = psum_pairs.tile([P, PACK, P], F32, tag="hidden")
         for t in range(PACK):
-            nc.tensor.transpose(out=b2_turned[:, t, :], in_=b2_sorted[:, t, :], identity=identity[:])
+            nc.tensor.transpose(out=b2_turned[:, t, :], in_=b2_rows_f32[:, t, :], identity=identity[:])
         b2_cols = consts.tile([P, PACK, N], F32)
         nc.vector.tensor_copy(out=b2_cols[:], in_=b2_turned[:, :, 0:N])
 
@@ -150,20 +150,20 @@ def tile_neuronpool_pa_kernel(tc, h1, W2, b2, W3, b3, gamma, beta, tick, out):
             quantise("x", n, tiles["x_grouped", n][:].rearrange("p b t -> p (b t)"), B)
 
         def regroup_w2_on_scalar(n):
-            w2_grouped = make(work, "w2_grouped", n, [P, PACK, P, PACK], BF16)
+            w2_grouped = make(work, "w2_grouped", n, [P, HID, PACK], BF16)
             nc.scalar.copy(
-                out=w2_grouped[:].rearrange("p i c t -> p c t i")[:, :W2_SCALAR_WORDS],
-                in_=rows_in_runs(tiles["w2_rows", n][:])[:, :W2_SCALAR_WORDS],
+                out=words_in_runs(w2_grouped[:])[:, :W2_SCALAR_RUNS],
+                in_=rows_in_runs(tiles["w2_rows", n][:])[:, :W2_SCALAR_RUNS],
             )
 
         def regroup_w2_on_vector(n):
             nc.vector.tensor_copy(
-                out=tiles["w2_grouped", n][:].rearrange("p i c t -> p c t i")[:, W2_SCALAR_WORDS:],
-                in_=rows_in_runs(tiles["w2_rows", n][:])[:, W2_SCALAR_WORDS:],
+                out=words_in_runs(tiles["w2_grouped", n][:])[:, W2_SCALAR_RUNS:],
+                in_=rows_in_runs(tiles["w2_rows", n][:])[:, W2_SCALAR_RUNS:],
             )
 
         def quantise_w2(n):
-            quantise("w2", n, tiles["w2_grouped", n][:].rearrange("p i c t -> p (i c t)"), HID)
+            quantise("w2", n, tiles["w2_grouped", n][:].rearrange("p j t -> p (j t)"), HID)
 
         def regroup_w3(n):
             w3_grouped = make(work, "w3_grouped", n, [P, D, PACK], BF16)

@@ -20,9 +20,8 @@ FMIN, FMAX, TICK_INTERVAL = 0.5, 40.0, 0.1
 PI = 3.141592653589793
 SINE_TERMS = 16
 
-GROUP = 4
 RUN = 4
-W2_SCALAR_RUNS = 96
+W2_SCALAR_RUNS = 104
 FIRST_STEP, LAST_STEP = -2, N + 3
 LOADS_AHEAD = 4
 LOAD_BUFS = LOADS_AHEAD + 3
@@ -87,9 +86,8 @@ def tile_neuronpool_pa_kernel(tc, h1, W2, b2, W3, b3, gamma, beta, tick, out):
             nc.sync.dma_start(out=ln_rows[v * N : (v + 1) * N, :], in_=vector)
 
         def load(n):
-            if n % GROUP == 0:
-                x_rows = make(loads, "x_rows", n // GROUP, [P, GROUP, HID], BF16)
-                nc.sync.dma_start(out=x_rows[:], in_=h1[:, n : n + GROUP, :])
+            x_rows = make(loads, "x_rows", n, [P, HID], BF16)
+            nc.sync.dma_start(out=x_rows[:], in_=h1[:, n, :])
             w2_rows = make(loads, "w2_rows", n, [P, PACK, HID], BF16)
             nc.sync.dma_start(out=w2_rows[:], in_=W2[n].rearrange("(p t) j -> p t j", t=PACK))
             w3_rows = make(loads, "w3_rows", n, [P, PACK, D], BF16)
@@ -131,8 +129,7 @@ def tile_neuronpool_pa_kernel(tc, h1, W2, b2, W3, b3, gamma, beta, tick, out):
             nc.vector.quantize_mx(out=codes[:].bitcast(FP8X4), scales=scales[:], in_=grouped)
 
         def turn_x(n):
-            x_rows = tiles["x_rows", n // GROUP]
-            x_words = x_rows[:, n % GROUP, :].bitcast(F32).rearrange("b (p u) -> b u p", u=2)
+            x_words = tiles["x_rows", n][:].bitcast(F32).rearrange("b (p u) -> b u p", u=2)
             x_turned = make_bank(psum_single, "x_turned", n, [P, 2, B])
             for u in range(2):
                 nc.tensor.transpose(out=x_turned[:, u, :], in_=x_words[:, u, :], identity=identity[:])
@@ -292,19 +289,16 @@ def tile_neuronpool_pa_kernel(tc, h1, W2, b2, W3, b3, gamma, beta, tick, out):
             )
 
         def finish(n):
-            if n % GROUP == 0:
-                make(work, "results", n // GROUP, [P, GROUP, D], F32)
-            results = tiles["results", n // GROUP]
+            result = make(work, "result", n, [P, D], F32)
             nc.vector.scalar_tensor_tensor(
-                out=results[:, n % GROUP, :],
+                out=result[:],
                 in0=tiles["centred", n][:],
                 scalar=tiles["rstd_gain", n][:],
                 in1=tiles["beta_spread", n][:],
                 op0=ALU.mult,
                 op1=ALU.add,
             )
-            if n % GROUP == GROUP - 1:
-                nc.sync.dma_start(out=out[:, n - GROUP + 1 : n + 1, :], in_=results[:])
+            nc.sync.dma_start(out=out[:, n, :], in_=result[:])
 
         def run(stage, n):
             if 0 <= n < N:

@@ -24,6 +24,7 @@ RUN = 4
 W2_SCALAR_RUNS = 104
 FIRST_STEP, LAST_STEP = -2, N + 3
 LOADS_AHEAD = 4
+B3_CHUNK = 8
 LOAD_BUFS = LOADS_AHEAD + 3
 
 FLOPS = 2 * B * N * HID * (HID + D)
@@ -85,6 +86,14 @@ def tile_neuronpool_pa_kernel(tc, h1, W2, b2, W3, b3, gamma, beta, tick, out):
         for v, vector in enumerate((b3, gamma, beta)):
             nc.sync.dma_start(out=ln_rows[v * N : (v + 1) * N, :], in_=vector)
 
+        b3_all = consts.tile([P, N, D], BF16)
+
+        def load_b3(first):
+            nc.sync.dma_start(
+                out=b3_all[:, first : first + B3_CHUNK, :],
+                in_=b3[first : first + B3_CHUNK, :].partition_broadcast(P),
+            )
+
         def load(n):
             x_rows = make(loads, "x_rows", n, [P, HID], BF16)
             nc.sync.dma_start(out=x_rows[:], in_=h1[:, n, :])
@@ -92,9 +101,12 @@ def tile_neuronpool_pa_kernel(tc, h1, W2, b2, W3, b3, gamma, beta, tick, out):
             nc.sync.dma_start(out=w2_rows[:], in_=W2[n].rearrange("(p t) j -> p t j", t=PACK))
             w3_rows = make(loads, "w3_rows", n, [P, PACK, D], BF16)
             nc.sync.dma_start(out=w3_rows[:], in_=W3[n].rearrange("(t p) d -> p t d", p=P))
+            if n % B3_CHUNK == 0 and n > 0:
+                load_b3(n)
 
         for n in range(LOADS_AHEAD):
             load(n)
+        load_b3(0)
 
         b2_rows_f32 = consts.tile([P, PACK, P], F32)
         nc.vector.tensor_copy(out=b2_rows_f32[:], in_=b2_rows[:].rearrange("n (t p) -> n t p", p=P))
@@ -216,12 +228,6 @@ def tile_neuronpool_pa_kernel(tc, h1, W2, b2, W3, b3, gamma, beta, tick, out):
                 stop=True,
             )
 
-        def spread_b3(n):
-            spread(make_bank(psum_single, "b3_spread", n, [P, D]), ln_cols, n)
-
-        def copy_b3(n):
-            nc.scalar.copy(out=make(work, "b3_all", n, [P, D], F32)[:], in_=tiles["b3_spread", n][:])
-
         def spread_gamma(n):
             spread(make_bank(psum_single, "gamma_spread", n, [P, D]), ln_cols, N + n)
 
@@ -240,7 +246,7 @@ def tile_neuronpool_pa_kernel(tc, h1, W2, b2, W3, b3, gamma, beta, tick, out):
                 out=make(work, "y", n, [P, D], F32)[:],
                 in0=tiles["y_sums", n][:],
                 scalar=1.0,
-                in1=tiles["b3_all", n][:],
+                in1=b3_all[:, n, :],
                 op0=ALU.mult,
                 op1=ALU.add,
                 accum_out=make(work, "y_total", n, [P, 1], F32)[:],
@@ -312,7 +318,6 @@ def tile_neuronpool_pa_kernel(tc, h1, W2, b2, W3, b3, gamma, beta, tick, out):
             run(regroup_w3, k)
             run(add_b3, k - 3)
             run(spread_beta, k - 4)
-            run(spread_b3, k - 2)
             run(regroup_w2_on_vector, k)
             run(take_mean, k - 3)
             run(copy_x, k + 1)
@@ -328,5 +333,4 @@ def tile_neuronpool_pa_kernel(tc, h1, W2, b2, W3, b3, gamma, beta, tick, out):
             run(finish, k - 4)
             run(quantise_g, k - 2)
             run(second_layer, k - 2)
-            run(copy_b3, k - 2)
             run(quantise_w2, k)

@@ -21,11 +21,15 @@ PI = 3.141592653589793
 SINE_TERMS = 16
 
 RUN = 4
-W2_SCALAR_RUNS = 104
-FIRST_STEP, LAST_STEP = -2, N + 3
+W2_SCALAR_RUNS = 112
+W2_SCALAR_RUNS_FIRST = 64
+FIRST_STEP = -2
 LOADS_AHEAD = 4
 B3_CHUNK = 8
 LOAD_BUFS = LOADS_AHEAD + 3
+
+GROUP_SIZES = [4] * 7 + [2] * 2
+GROUP_OF = [(sum(GROUP_SIZES[:g]), size) for g, size in enumerate(GROUP_SIZES) for j in range(size)]
 
 FLOPS = 2 * B * N * HID * (HID + D)
 
@@ -59,6 +63,7 @@ def tile_neuronpool_pa_kernel(tc, h1, W2, b2, W3, b3, gamma, beta, tick, out):
         consts = stack.enter_context(tc.tile_pool(name="consts", bufs=1))
         loads = stack.enter_context(tc.tile_pool(name="loads", bufs=LOAD_BUFS))
         work = stack.enter_context(tc.tile_pool(name="work", bufs=4))
+        ln = stack.enter_context(tc.tile_pool(name="ln", bufs=8))
         psum_pairs = stack.enter_context(tc.psum_pool(name="psum_pairs", bufs=2))
         psum_single = stack.enter_context(tc.psum_pool(name="psum_single", bufs=1))
         stack.enter_context(tc.manual_schedule())
@@ -75,16 +80,19 @@ def tile_neuronpool_pa_kernel(tc, h1, W2, b2, W3, b3, gamma, beta, tick, out):
 
         identity = consts.tile([P, P], F32)
         make_identity(nc, identity[:])
-        minus_half = consts.tile([P, 1], F32)
+        minus_half = consts.tile([P, max(GROUP_SIZES)], F32)
         nc.vector.memset(minus_half[:], -0.5)
 
         b2_rows = consts.tile([P, HID], BF16)
         nc.vector.memset(b2_rows[:], 0.0)
-        nc.sync.dma_start(out=b2_rows[0:N, :], in_=b2)
+        nc.scalar.dma_start(out=b2_rows[0:N, :], in_=b2)
         ln_rows = consts.tile([P, D], BF16)
         nc.vector.memset(ln_rows[:], 0.0)
-        for v, vector in enumerate((b3, gamma, beta)):
-            nc.sync.dma_start(out=ln_rows[v * N : (v + 1) * N, :], in_=vector)
+        for v, vector in enumerate((gamma, beta)):
+            nc.scalar.dma_start(out=ln_rows[v * N : (v + 1) * N, :], in_=vector)
+        b2_cols = consts.tile([P, PACK, N], F32)
+        ln_cols = consts.tile([P, D_HALVES, P], F32)
+        ln_gain_cols = consts.tile([P, D_HALVES, 2, N], F32)
 
         b3_all = consts.tile([P, N, D], BF16)
 
@@ -108,31 +116,36 @@ def tile_neuronpool_pa_kernel(tc, h1, W2, b2, W3, b3, gamma, beta, tick, out):
             load(n)
         load_b3(0)
 
-        b2_rows_f32 = consts.tile([P, PACK, P], F32)
-        nc.vector.tensor_copy(out=b2_rows_f32[:], in_=b2_rows[:].rearrange("n (t p) -> n t p", p=P))
-        b2_turned = psum_pairs.tile([P, PACK, P], F32, tag="hidden")
-        for t in range(PACK):
-            nc.tensor.transpose(out=b2_turned[:, t, :], in_=b2_rows_f32[:, t, :], identity=identity[:])
-        b2_cols = consts.tile([P, PACK, N], F32)
-        nc.vector.tensor_copy(out=b2_cols[:], in_=b2_turned[:, :, 0:N])
-
-        ln_rows_f32 = consts.tile([P, D], F32)
-        nc.vector.tensor_copy(out=ln_rows_f32[:], in_=ln_rows[:])
-        ln_turned = psum_single.tile([P, D_HALVES, P], F32, tag="x_turned")
-        for h in range(D_HALVES):
-            nc.tensor.transpose(
-                out=ln_turned[:, h, :], in_=ln_rows_f32[:, h * P : (h + 1) * P], identity=identity[:]
-            )
-        ln_cols = consts.tile([P, D_HALVES, P], F32)
-        nc.vector.tensor_copy(out=ln_cols[:], in_=ln_turned[:])
-        beta_gain_cols = consts.tile([P, D_HALVES, N], F32)
-
-        def spread(dst, cols, column):
+        def turn_vectors():
+            b2_rows_f32 = consts.tile([P, PACK, P], F32)
+            nc.vector.tensor_copy(out=b2_rows_f32[:], in_=b2_rows[:].rearrange("n (t p) -> n t p", p=P))
+            tiles["b2_turned"] = psum_pairs.tile([P, PACK, P], F32, name="hidden")
+            for t in range(PACK):
+                nc.tensor.transpose(
+                    out=tiles["b2_turned"][:, t, :], in_=b2_rows_f32[:, t, :], identity=identity[:]
+                )
+            ln_rows_f32 = consts.tile([P, D], F32)
+            nc.vector.tensor_copy(out=ln_rows_f32[:], in_=ln_rows[:])
+            tiles["ln_turned"] = psum_pairs.tile([P, D_HALVES, P], F32, name="ln_all")
             for h in range(D_HALVES):
                 nc.tensor.transpose(
-                    out=dst[:, h * P : (h + 1) * P],
-                    in_=cols[:, h, column : column + 1].to_broadcast([P, P]),
+                    out=tiles["ln_turned"][:, h, :],
+                    in_=ln_rows_f32[:, h * P : (h + 1) * P],
                     identity=identity[:],
+                )
+
+        def keep_vectors():
+            nc.vector.tensor_copy(out=b2_cols[:], in_=tiles["b2_turned"][:, :, 0:N])
+            nc.vector.tensor_copy(out=ln_cols[:], in_=tiles["ln_turned"][:])
+            ln_by_vector = ln_cols[:].rearrange("p h (v n) -> p h v n", n=N)
+            for n in range(N):
+                nc.gpsimd.tensor_scalar(
+                    out=ln_gain_cols[:, :, :, n : n + 1],
+                    in0=ln_by_vector[:, :, 0:2, n : n + 1],
+                    scalar1=oscillator_gain(n, tick),
+                    scalar2=0.0,
+                    op0=ALU.mult,
+                    op1=ALU.add,
                 )
 
         def quantise(name, n, grouped, width):
@@ -158,17 +171,20 @@ def tile_neuronpool_pa_kernel(tc, h1, W2, b2, W3, b3, gamma, beta, tick, out):
         def quantise_x(n):
             quantise("x", n, tiles["x_grouped", n][:].rearrange("p b t -> p (b t)"), B)
 
+        def scalar_runs(n):
+            return W2_SCALAR_RUNS if n > 0 else W2_SCALAR_RUNS_FIRST
+
         def regroup_w2_on_scalar(n):
             w2_grouped = make(work, "w2_grouped", n, [P, HID, PACK], BF16)
             nc.scalar.copy(
-                out=words_in_runs(w2_grouped[:])[:, :W2_SCALAR_RUNS],
-                in_=rows_in_runs(tiles["w2_rows", n][:])[:, :W2_SCALAR_RUNS],
+                out=words_in_runs(w2_grouped[:])[:, : scalar_runs(n)],
+                in_=rows_in_runs(tiles["w2_rows", n][:])[:, : scalar_runs(n)],
             )
 
         def regroup_w2_on_vector(n):
             nc.vector.tensor_copy(
-                out=words_in_runs(tiles["w2_grouped", n][:])[:, W2_SCALAR_RUNS:],
-                in_=rows_in_runs(tiles["w2_rows", n][:])[:, W2_SCALAR_RUNS:],
+                out=words_in_runs(tiles["w2_grouped", n][:])[:, scalar_runs(n) :],
+                in_=rows_in_runs(tiles["w2_rows", n][:])[:, scalar_runs(n) :],
             )
 
         def quantise_w2(n):
@@ -228,33 +244,34 @@ def tile_neuronpool_pa_kernel(tc, h1, W2, b2, W3, b3, gamma, beta, tick, out):
                 stop=True,
             )
 
-        def spread_gamma(n):
-            spread(make_bank(psum_single, "gamma_spread", n, [P, D]), ln_cols, N + n)
+        def spread(n, kind="ln_all"):
+            ln_all = psum_pairs.tile([P, 2, D], F32, name=kind)
+            tiles["ln_all", n] = ln_all
+            for v in range(2):
+                for h in range(D_HALVES):
+                    nc.tensor.transpose(
+                        out=ln_all[:, v, h * P : (h + 1) * P],
+                        in_=ln_gain_cols[:, h, v, n : n + 1].to_broadcast([P, P]),
+                        identity=identity[:],
+                    )
 
-        def scale_beta(n):
-            nc.scalar.mul(
-                out=beta_gain_cols[:, :, n : n + 1],
-                in_=ln_cols[:, :, 2 * N + n : 2 * N + n + 1],
-                mul=oscillator_gain(n, tick),
-            )
-
-        def spread_beta(n):
-            spread(make_bank(psum_single, "beta_spread", n, [P, D]), beta_gain_cols, n)
+        def column(name, n):
+            first, size = GROUP_OF[n]
+            return tiles[name, first][:, n - first : n - first + 1]
 
         def add_b3(n):
+            first, size = GROUP_OF[n]
+            if n == first:
+                make(work, "y_totals", first, [P, size], F32)
+                make(work, "square_totals", first, [P, size], F32)
             nc.vector.scalar_tensor_tensor(
-                out=make(work, "y", n, [P, D], F32)[:],
+                out=make(ln, "y", n, [P, D], F32)[:],
                 in0=tiles["y_sums", n][:],
                 scalar=1.0,
                 in1=b3_all[:, n, :],
                 op0=ALU.mult,
                 op1=ALU.add,
-                accum_out=make(work, "y_total", n, [P, 1], F32)[:],
-            )
-
-        def take_mean(n):
-            nc.vector.tensor_scalar_mul(
-                out=make(work, "mean", n, [P, 1], F32)[:], in0=tiles["y_total", n][:], scalar1=1.0 / D
+                accum_out=column("y_totals", n),
             )
 
         def sum_squares(n):
@@ -262,34 +279,45 @@ def tile_neuronpool_pa_kernel(tc, h1, W2, b2, W3, b3, gamma, beta, tick, out):
                 out=make(work, "squares", n, [P, D], F32)[:],
                 in_=tiles["y", n][:],
                 func=ACT.Square,
-                bias=tiles["mean", n][:],
-                scale=-1.0,
-                accum_out=make(work, "square_total", n, [P, 1], F32)[:],
+                bias=column("y_totals", n),
+                scale=-float(D),
+                accum_out=column("square_totals", n),
             )
 
-        def take_rstd(n):
-            gain = oscillator_gain(n, tick)
+        def take_rstds(n):
+            first, size = GROUP_OF[n]
+            if n != first + size - 1:
+                return
             nc.gpsimd.tensor_scalar(
-                out=make(work, "scaled_var", n, [P, 1], F32)[:],
-                in0=tiles["square_total", n][:],
-                scalar1=1.0 / (D * gain * gain),
-                scalar2=LN_EPS / (gain * gain),
+                out=make(work, "var_eps", first, [P, size], F32)[:],
+                in0=tiles["square_totals", first][:],
+                scalar1=1.0 / D**3,
+                scalar2=LN_EPS,
                 op0=ALU.mult,
                 op1=ALU.add,
             )
             nc.gpsimd.tensor_tensor(
-                out=make(work, "rstd_gain", n, [P, 1], F32)[:],
-                in0=tiles["scaled_var", n][:],
-                in1=minus_half[:],
+                out=make(work, "rstds", first, [P, size], F32)[:],
+                in0=tiles["var_eps", first][:],
+                in1=minus_half[:, 0:size],
                 op=ALU.pow,
             )
+
+        def take_means(n):
+            first, size = GROUP_OF[n]
+            if n == first + size - 1:
+                nc.vector.tensor_scalar_mul(
+                    out=make(work, "means", first, [P, size], F32)[:],
+                    in0=tiles["y_totals", first][:],
+                    scalar1=1.0 / D,
+                )
 
         def centre(n):
             nc.vector.scalar_tensor_tensor(
                 out=make(work, "centred", n, [P, D], F32)[:],
                 in0=tiles["y", n][:],
-                scalar=tiles["mean", n][:],
-                in1=tiles["gamma_spread", n][:],
+                scalar=column("means", n),
+                in1=tiles["ln_all", n][:, 0, :],
                 op0=ALU.subtract,
                 op1=ALU.mult,
             )
@@ -299,8 +327,8 @@ def tile_neuronpool_pa_kernel(tc, h1, W2, b2, W3, b3, gamma, beta, tick, out):
             nc.vector.scalar_tensor_tensor(
                 out=result[:],
                 in0=tiles["centred", n][:],
-                scalar=tiles["rstd_gain", n][:],
-                in1=tiles["beta_spread", n][:],
+                scalar=column("rstds", n),
+                in1=tiles["ln_all", n][:, 1, :],
                 op0=ALU.mult,
                 op1=ALU.add,
             )
@@ -310,27 +338,60 @@ def tile_neuronpool_pa_kernel(tc, h1, W2, b2, W3, b3, gamma, beta, tick, out):
             if 0 <= n < N:
                 stage(n)
 
-        for k in range(FIRST_STEP, LAST_STEP + 1):
+        for k in range(FIRST_STEP, N):
             run(load, k - FIRST_STEP + LOADS_AHEAD)
             run(first_layer, k - 1)
             run(regroup_w2_on_scalar, k)
-            run(scale_beta, k)
-            run(regroup_w3, k)
-            run(add_b3, k - 3)
-            run(spread_beta, k - 4)
             run(regroup_w2_on_vector, k)
-            run(take_mean, k - 3)
+            run(regroup_w3, k)
+            if k == 0:
+                turn_vectors()
+            run(finish, k - 8)
+            run(add_b3, k - 3)
+            run(centre, k - 7)
             run(copy_x, k + 1)
             run(regroup_g, k - 2)
-            run(centre, k - 3)
             run(sum_squares, k - 3)
-            run(take_rstd, k - 3)
-            run(spread_gamma, k - 2)
+            run(take_rstds, k - 3)
+            run(spread, k - 6)
             run(turn_x, k + 2)
             run(quantise_w3, k)
             run(quantise_x, k)
+            if k == 0:
+                keep_vectors()
             run(gelu, k - 1)
-            run(finish, k - 4)
+            run(take_means, k - 3)
             run(quantise_g, k - 2)
             run(second_layer, k - 2)
             run(quantise_w2, k)
+
+        first_layer(N - 1)
+        gelu(N - 1)
+        regroup_g(N - 2)
+        add_b3(N - 3)
+        sum_squares(N - 3)
+        take_rstds(N - 3)
+        finish(N - 8)
+        quantise_g(N - 2)
+        second_layer(N - 2)
+        centre(N - 7)
+        spread(N - 6)
+        regroup_g(N - 1)
+        finish(N - 7)
+        quantise_g(N - 1)
+        second_layer(N - 1)
+        add_b3(N - 2)
+        sum_squares(N - 2)
+        take_means(N - 3)
+        centre(N - 6)
+        add_b3(N - 1)
+        sum_squares(N - 1)
+        take_rstds(N - 1)
+        finish(N - 6)
+        take_means(N - 1)
+        for n in range(N - 5, N):
+            spread(n, kind="hidden" if n >= N - 2 else "ln_all")
+            centre(n)
+            if n > N - 5:
+                finish(n - 1)
+        finish(N - 1)

@@ -21,12 +21,12 @@ PI = 3.141592653589793
 SINE_TERMS = 16
 
 RUN = 4
-W2_SCALAR_RUNS = 112
+W2_SCALAR_RUNS = 106
 W2_SCALAR_RUNS_FIRST = 64
-FIRST_STEP = -2
+FIRST_STEP = -3
 LOADS_AHEAD = 4
 B3_CHUNK = 8
-LOAD_BUFS = LOADS_AHEAD + 3
+LOAD_BUFS = LOADS_AHEAD + 4
 
 GROUP_SIZES = [4] * 7 + [2] * 2
 GROUP_OF = [(sum(GROUP_SIZES[:g]), size) for g, size in enumerate(GROUP_SIZES) for j in range(size)]
@@ -65,7 +65,6 @@ def tile_neuronpool_pa_kernel(tc, h1, W2, b2, W3, b3, gamma, beta, tick, out):
         work = stack.enter_context(tc.tile_pool(name="work", bufs=4))
         ln = stack.enter_context(tc.tile_pool(name="ln", bufs=8))
         psum_pairs = stack.enter_context(tc.psum_pool(name="psum_pairs", bufs=2))
-        psum_single = stack.enter_context(tc.psum_pool(name="psum_single", bufs=1))
         stack.enter_context(tc.manual_schedule())
 
         tiles = {}
@@ -82,17 +81,18 @@ def tile_neuronpool_pa_kernel(tc, h1, W2, b2, W3, b3, gamma, beta, tick, out):
         make_identity(nc, identity[:])
         minus_half = consts.tile([P, max(GROUP_SIZES)], F32)
         nc.vector.memset(minus_half[:], -0.5)
+        ones = consts.tile([P, 1], F32)
+        nc.vector.memset(ones[:], 1.0)
 
         b2_rows = consts.tile([P, HID], BF16)
         nc.vector.memset(b2_rows[:], 0.0)
-        nc.scalar.dma_start(out=b2_rows[0:N, :], in_=b2)
         ln_rows = consts.tile([P, D], BF16)
         nc.vector.memset(ln_rows[:], 0.0)
-        for v, vector in enumerate((gamma, beta)):
-            nc.scalar.dma_start(out=ln_rows[v * N : (v + 1) * N, :], in_=vector)
         b2_cols = consts.tile([P, PACK, N], F32)
-        ln_cols = consts.tile([P, D_HALVES, P], F32)
         ln_gain_cols = consts.tile([P, D_HALVES, 2, N], F32)
+        gains = consts.tile([P, N], F32)
+        for n in range(N):
+            nc.scalar.mul(out=gains[:, n : n + 1], in_=ones[:], mul=oscillator_gain(n, tick))
 
         b3_all = consts.tile([P, N, D], BF16)
 
@@ -102,19 +102,37 @@ def tile_neuronpool_pa_kernel(tc, h1, W2, b2, W3, b3, gamma, beta, tick, out):
                 in_=b3[first : first + B3_CHUNK, :].partition_broadcast(P),
             )
 
-        def load(n):
+        def load_vectors():
+            nc.sync.dma_start(out=b2_rows[0:N, :], in_=b2)
+            for v, vector in enumerate((gamma, beta)):
+                nc.sync.dma_start(out=ln_rows[v * N : (v + 1) * N, :], in_=vector)
+
+        def load_x(n):
             x_rows = make(loads, "x_rows", n, [P, HID], BF16)
             nc.sync.dma_start(out=x_rows[:], in_=h1[:, n, :])
+
+        def load_w2(n):
             w2_rows = make(loads, "w2_rows", n, [P, PACK, HID], BF16)
             nc.sync.dma_start(out=w2_rows[:], in_=W2[n].rearrange("(p t) j -> p t j", t=PACK))
+
+        def load_w3(n):
             w3_rows = make(loads, "w3_rows", n, [P, PACK, D], BF16)
             nc.sync.dma_start(out=w3_rows[:], in_=W3[n].rearrange("(t p) d -> p t d", p=P))
-            if n % B3_CHUNK == 0 and n > 0:
-                load_b3(n)
+            if n % B3_CHUNK == 2:
+                load_b3(n - 2)
 
-        for n in range(LOADS_AHEAD):
-            load(n)
-        load_b3(0)
+        load_x(0)
+        load_w2(0)
+        load_vectors()
+        load_x(1)
+        load_w2(1)
+        load_x(2)
+        load_w2(2)
+        load_x(3)
+        load_w3(0)
+        load_w2(3)
+        load_x(4)
+        load_w3(1)
 
         def turn_vectors():
             b2_rows_f32 = consts.tile([P, PACK, P], F32)
@@ -136,16 +154,13 @@ def tile_neuronpool_pa_kernel(tc, h1, W2, b2, W3, b3, gamma, beta, tick, out):
 
         def keep_vectors():
             nc.vector.tensor_copy(out=b2_cols[:], in_=tiles["b2_turned"][:, :, 0:N])
-            nc.vector.tensor_copy(out=ln_cols[:], in_=tiles["ln_turned"][:])
-            ln_by_vector = ln_cols[:].rearrange("p h (v n) -> p h v n", n=N)
-            for n in range(N):
-                nc.gpsimd.tensor_scalar(
-                    out=ln_gain_cols[:, :, :, n : n + 1],
-                    in0=ln_by_vector[:, :, 0:2, n : n + 1],
-                    scalar1=oscillator_gain(n, tick),
-                    scalar2=0.0,
-                    op0=ALU.mult,
-                    op1=ALU.add,
+            ln_by_vector = tiles["ln_turned"][:].rearrange("p h (v n) -> p h v n", n=N)
+            for v in range(2):
+                nc.vector.tensor_tensor(
+                    out=ln_gain_cols[:, :, v, :],
+                    in0=ln_by_vector[:, :, v, :],
+                    in1=gains[:].unsqueeze(1).to_broadcast([P, D_HALVES, N]),
+                    op=ALU.mult,
                 )
 
         def quantise(name, n, grouped, width):
@@ -155,7 +170,7 @@ def tile_neuronpool_pa_kernel(tc, h1, W2, b2, W3, b3, gamma, beta, tick, out):
 
         def turn_x(n):
             x_words = tiles["x_rows", n][:].bitcast(F32).rearrange("b (p u) -> b u p", u=2)
-            x_turned = make_bank(psum_single, "x_turned", n, [P, 2, B])
+            x_turned = make_bank(psum_pairs, "x_turned", n, [P, 2, B])
             for u in range(2):
                 nc.tensor.transpose(out=x_turned[:, u, :], in_=x_words[:, u, :], identity=identity[:])
 
@@ -323,7 +338,7 @@ def tile_neuronpool_pa_kernel(tc, h1, W2, b2, W3, b3, gamma, beta, tick, out):
             )
 
         def finish(n):
-            result = make(work, "result", n, [P, D], F32)
+            result = make(ln, "result", n, [P, D], F32)
             nc.vector.scalar_tensor_tensor(
                 out=result[:],
                 in0=tiles["centred", n][:],
@@ -339,59 +354,79 @@ def tile_neuronpool_pa_kernel(tc, h1, W2, b2, W3, b3, gamma, beta, tick, out):
                 stage(n)
 
         for k in range(FIRST_STEP, N):
-            run(load, k - FIRST_STEP + LOADS_AHEAD)
+            run(load_x, k + 8)
+            run(load_w2, k + 7)
+            run(load_w3, k + 5)
+            run(turn_x, k + 3)
+            run(spread, k - 8)
+            run(second_layer, k - 3)
             run(first_layer, k - 1)
-            run(regroup_w2_on_scalar, k)
-            run(regroup_w2_on_vector, k)
-            run(regroup_w3, k)
-            if k == 0:
-                turn_vectors()
-            run(finish, k - 8)
-            run(add_b3, k - 3)
-            run(centre, k - 7)
-            run(copy_x, k + 1)
-            run(regroup_g, k - 2)
-            run(sum_squares, k - 3)
-            run(take_rstds, k - 3)
-            run(spread, k - 6)
-            run(turn_x, k + 2)
-            run(quantise_w3, k)
-            run(quantise_x, k)
-            if k == 0:
-                keep_vectors()
+            run(regroup_w2_on_scalar, k + 1)
+            run(copy_x, k + 2)
+            run(sum_squares, k - 4)
+            run(take_rstds, k - 4)
             run(gelu, k - 1)
-            run(take_means, k - 3)
+            if k == -2:
+                turn_vectors()
+            run(quantise_x, k + 0)
+            run(quantise_w3, k - 2)
+            run(regroup_g, k - 2)
+            run(regroup_w2_on_vector, k + 1)
+            run(finish, k - 9)
+            run(add_b3, k - 3)
+            run(centre, k - 8)
+            run(take_means, k - 4)
+            run(regroup_w3, k - 1)
+            if k == -1:
+                keep_vectors()
             run(quantise_g, k - 2)
-            run(second_layer, k - 2)
-            run(quantise_w2, k)
+            run(quantise_w2, k + 0)
 
+        spread(N - 8)
+        second_layer(N - 3)
         first_layer(N - 1)
+        sum_squares(N - 4)
         gelu(N - 1)
+        quantise_w3(N - 2)
         regroup_g(N - 2)
+        finish(N - 9)
         add_b3(N - 3)
         sum_squares(N - 3)
         take_rstds(N - 3)
-        finish(N - 8)
         quantise_g(N - 2)
         second_layer(N - 2)
-        centre(N - 7)
+        centre(N - 8)
+        spread(N - 7)
+        regroup_w3(N - 1)
+        take_means(N - 3)
+        finish(N - 8)
         spread(N - 6)
         regroup_g(N - 1)
-        finish(N - 7)
+        centre(N - 7)
+        quantise_w3(N - 1)
         quantise_g(N - 1)
         second_layer(N - 1)
         add_b3(N - 2)
         sum_squares(N - 2)
-        take_means(N - 3)
-        centre(N - 6)
+        finish(N - 7)
+        spread(N - 5)
         add_b3(N - 1)
         sum_squares(N - 1)
         take_rstds(N - 1)
-        finish(N - 6)
+        centre(N - 6)
         take_means(N - 1)
-        for n in range(N - 5, N):
-            spread(n, kind="hidden" if n >= N - 2 else "ln_all")
-            centre(n)
-            if n > N - 5:
-                finish(n - 1)
+        finish(N - 6)
+        spread(N - 4)
+        centre(N - 5)
+        finish(N - 5)
+        spread(N - 3)
+        centre(N - 4)
+        finish(N - 4)
+        spread(N - 2)
+        centre(N - 3)
+        finish(N - 3)
+        spread(N - 1)
+        centre(N - 2)
+        finish(N - 2)
+        centre(N - 1)
         finish(N - 1)

@@ -25,7 +25,7 @@ W2_SCALAR_RUNS = 106
 W2_SCALAR_RUNS_FIRST = 64
 FIRST_STEP = -3
 LOADS_AHEAD = 4
-B3_CHUNK = 8
+B3_GROUP = 4
 LOAD_BUFS = LOADS_AHEAD + 4
 
 GROUP_SIZES = [4] * 7 + [2] * 2
@@ -65,6 +65,7 @@ def tile_neuronpool_pa_kernel(tc, h1, W2, b2, W3, b3, gamma, beta, tick, out):
         work = stack.enter_context(tc.tile_pool(name="work", bufs=4))
         ln = stack.enter_context(tc.tile_pool(name="ln", bufs=8))
         psum_pairs = stack.enter_context(tc.psum_pool(name="psum_pairs", bufs=2))
+        psum_single = stack.enter_context(tc.psum_pool(name="psum_single", bufs=1))
         stack.enter_context(tc.manual_schedule())
 
         tiles = {}
@@ -79,6 +80,8 @@ def tile_neuronpool_pa_kernel(tc, h1, W2, b2, W3, b3, gamma, beta, tick, out):
 
         identity = consts.tile([P, P], F32)
         make_identity(nc, identity[:])
+        identity_bf16 = consts.tile([P, P], BF16)
+        nc.gpsimd.tensor_copy(out=identity_bf16[:], in_=identity[:])
         minus_half = consts.tile([P, max(GROUP_SIZES)], F32)
         nc.vector.memset(minus_half[:], -0.5)
         ones = consts.tile([P, 1], F32)
@@ -90,36 +93,29 @@ def tile_neuronpool_pa_kernel(tc, h1, W2, b2, W3, b3, gamma, beta, tick, out):
         nc.vector.memset(ln_rows[:], 0.0)
         b2_cols = consts.tile([P, PACK, N], F32)
         ln_gain_cols = consts.tile([P, D_HALVES, 2, N], F32)
+        b3_cols = consts.tile([P, D_HALVES, N], BF16)
         gains = consts.tile([P, N], F32)
+        nc.scalar.activation(out=gains[:, 0:1], in_=ones[:], func=ACT.Gelu, bias=0.0, scale=1.0)
         for n in range(N):
             nc.scalar.mul(out=gains[:, n : n + 1], in_=ones[:], mul=oscillator_gain(n, tick))
 
-        b3_all = consts.tile([P, N, D], BF16)
-
-        def load_b3(first):
-            nc.sync.dma_start(
-                out=b3_all[:, first : first + B3_CHUNK, :],
-                in_=b3[first : first + B3_CHUNK, :].partition_broadcast(P),
-            )
-
         def load_vectors():
             nc.sync.dma_start(out=b2_rows[0:N, :], in_=b2)
-            for v, vector in enumerate((gamma, beta)):
+            for v, vector in enumerate((gamma, beta, b3)):
                 nc.sync.dma_start(out=ln_rows[v * N : (v + 1) * N, :], in_=vector)
 
         def load_x(n):
-            x_rows = make(loads, "x_rows", n, [P, HID], BF16)
-            nc.sync.dma_start(out=x_rows[:], in_=h1[:, n, :])
+            if n % 2 == 0:
+                x_rows = make(loads, "x_rows", n, [P, 2, HID], BF16)
+                nc.sync.dma_start(out=x_rows[:], in_=h1[:, n : n + 2, :])
 
         def load_w2(n):
             w2_rows = make(loads, "w2_rows", n, [P, PACK, HID], BF16)
-            nc.sync.dma_start(out=w2_rows[:], in_=W2[n].rearrange("(p t) j -> p t j", t=PACK))
+            nc.sync.dma_start(out=w2_rows[:].rearrange("p (u e) j -> p u e j", u=2), in_=W2[n].rearrange("(u p e) j -> p u e j", u=2, e=2))
 
         def load_w3(n):
             w3_rows = make(loads, "w3_rows", n, [P, PACK, D], BF16)
             nc.sync.dma_start(out=w3_rows[:], in_=W3[n].rearrange("(t p) d -> p t d", p=P))
-            if n % B3_CHUNK == 2:
-                load_b3(n - 2)
 
         load_x(0)
         load_w2(0)
@@ -155,6 +151,7 @@ def tile_neuronpool_pa_kernel(tc, h1, W2, b2, W3, b3, gamma, beta, tick, out):
         def keep_vectors():
             nc.vector.tensor_copy(out=b2_cols[:], in_=tiles["b2_turned"][:, :, 0:N])
             ln_by_vector = tiles["ln_turned"][:].rearrange("p h (v n) -> p h v n", n=N)
+            nc.vector.tensor_copy(out=b3_cols[:], in_=ln_by_vector[:, :, 2, :])
             for v in range(2):
                 nc.vector.tensor_tensor(
                     out=ln_gain_cols[:, :, v, :],
@@ -169,7 +166,7 @@ def tile_neuronpool_pa_kernel(tc, h1, W2, b2, W3, b3, gamma, beta, tick, out):
             nc.vector.quantize_mx(out=codes[:].bitcast(FP8X4), scales=scales[:], in_=grouped)
 
         def turn_x(n):
-            x_words = tiles["x_rows", n][:].bitcast(F32).rearrange("b (p u) -> b u p", u=2)
+            x_words = tiles["x_rows", n - n % 2][:, n % 2, :].bitcast(F32).rearrange("b (u p) -> b u p", u=2)
             x_turned = make_bank(psum_pairs, "x_turned", n, [P, 2, B])
             for u in range(2):
                 nc.tensor.transpose(out=x_turned[:, u, :], in_=x_words[:, u, :], identity=identity[:])
@@ -187,7 +184,7 @@ def tile_neuronpool_pa_kernel(tc, h1, W2, b2, W3, b3, gamma, beta, tick, out):
             quantise("x", n, tiles["x_grouped", n][:].rearrange("p b t -> p (b t)"), B)
 
         def scalar_runs(n):
-            return W2_SCALAR_RUNS if n > 0 else W2_SCALAR_RUNS_FIRST
+            return 80 + (108 - 80) * n // (N - 1) // 2 * 2
 
         def regroup_w2_on_scalar(n):
             w2_grouped = make(work, "w2_grouped", n, [P, HID, PACK], BF16)
@@ -244,11 +241,18 @@ def tile_neuronpool_pa_kernel(tc, h1, W2, b2, W3, b3, gamma, beta, tick, out):
                 out=words_in_runs(g_grouped[:]), in_=rows_in_runs(tiles["g_rows", n][:])
             )
 
+        def regroup_g_on_scalar(n):
+            g_grouped = make(work, "g_grouped", n, [P, B, PACK], BF16)
+            nc.scalar.copy(out=words_in_runs(g_grouped[:]), in_=rows_in_runs(tiles["g_rows", n][:]))
+
+        def spread_late(n):
+            spread(n, kind="hidden")
+
         def quantise_g(n):
             quantise("g", n, tiles["g_grouped", n][:].rearrange("p b t -> p (b t)"), B)
 
         def second_layer(n):
-            y_sums = make_bank(psum_pairs, "y_sums", n, [P, D])
+            y_sums = make_bank(psum_single, "y_sums", n, [P, D])
             nc.tensor.matmul_mx(
                 out=y_sums[:],
                 lhsT=tiles["g_codes", n][:].bitcast(FP8X4),
@@ -258,6 +262,23 @@ def tile_neuronpool_pa_kernel(tc, h1, W2, b2, W3, b3, gamma, beta, tick, out):
                 start=True,
                 stop=True,
             )
+
+        def spread_b3(n):
+            if n % B3_GROUP == 0:
+                b3_spread = psum_single.tile([P, B3_GROUP, D], BF16, name="b3_spread")
+                tiles["b3_spread", n] = b3_spread
+                for j in range(B3_GROUP):
+                    for h in range(D_HALVES):
+                        nc.tensor.transpose(
+                            out=b3_spread[:, j, h * P : (h + 1) * P],
+                            in_=b3_cols[:, h, n + j : n + j + 1].to_broadcast([P, P]),
+                            identity=identity_bf16[:],
+                        )
+
+        def copy_b3(n):
+            if n % B3_GROUP == 0:
+                b3_all = make(work, "b3_all", n, [P, B3_GROUP, D], BF16)
+                nc.scalar.copy(out=b3_all[:], in_=tiles["b3_spread", n][:])
 
         def spread(n, kind="ln_all"):
             ln_all = psum_pairs.tile([P, 2, D], F32, name=kind)
@@ -283,7 +304,7 @@ def tile_neuronpool_pa_kernel(tc, h1, W2, b2, W3, b3, gamma, beta, tick, out):
                 out=make(ln, "y", n, [P, D], F32)[:],
                 in0=tiles["y_sums", n][:],
                 scalar=1.0,
-                in1=b3_all[:, n, :],
+                in1=tiles["b3_all", n - n % B3_GROUP][:, n % B3_GROUP, :],
                 op0=ALU.mult,
                 op1=ALU.add,
                 accum_out=column("y_totals", n),
@@ -357,57 +378,63 @@ def tile_neuronpool_pa_kernel(tc, h1, W2, b2, W3, b3, gamma, beta, tick, out):
             run(load_x, k + 8)
             run(load_w2, k + 7)
             run(load_w3, k + 5)
-            run(turn_x, k + 3)
-            run(spread, k - 8)
             run(second_layer, k - 3)
             run(first_layer, k - 1)
+            run(turn_x, k + 3)
+            run(spread_b3, k + 0)
+            run(spread, k - 8)
             run(regroup_w2_on_scalar, k + 1)
             run(copy_x, k + 2)
+            run(copy_b3, k - 1)
             run(sum_squares, k - 4)
-            run(take_rstds, k - 4)
             run(gelu, k - 1)
             if k == -2:
                 turn_vectors()
             run(quantise_x, k + 0)
-            run(quantise_w3, k - 2)
+            run(centre, k - 9)
             run(regroup_g, k - 2)
+            run(quantise_w3, k - 2)
+            run(take_rstds, k - 5)
             run(regroup_w2_on_vector, k + 1)
-            run(finish, k - 9)
             run(add_b3, k - 3)
-            run(centre, k - 8)
             run(take_means, k - 4)
             run(regroup_w3, k - 1)
             if k == -1:
                 keep_vectors()
+            run(finish, k - 9)
             run(quantise_g, k - 2)
             run(quantise_w2, k + 0)
 
-        spread(N - 8)
         second_layer(N - 3)
         first_layer(N - 1)
+        spread(N - 8)
         sum_squares(N - 4)
         gelu(N - 1)
-        quantise_w3(N - 2)
+        centre(N - 9)
         regroup_g(N - 2)
-        finish(N - 9)
+        quantise_w3(N - 2)
+        take_rstds(N - 5)
         add_b3(N - 3)
         sum_squares(N - 3)
-        take_rstds(N - 3)
+        regroup_w3(N - 1)
         quantise_g(N - 2)
         second_layer(N - 2)
-        centre(N - 8)
+        finish(N - 9)
         spread(N - 7)
-        regroup_w3(N - 1)
-        take_means(N - 3)
-        finish(N - 8)
-        spread(N - 6)
+        centre(N - 8)
         regroup_g(N - 1)
-        centre(N - 7)
+        take_rstds(N - 3)
+        take_means(N - 3)
         quantise_w3(N - 1)
-        quantise_g(N - 1)
-        second_layer(N - 1)
         add_b3(N - 2)
         sum_squares(N - 2)
+        quantise_g(N - 1)
+        second_layer(N - 1)
+        finish(N - 8)
+        spread(N - 6)
+        spread_late(N - 2)
+        spread_late(N - 1)
+        centre(N - 7)
         finish(N - 7)
         spread(N - 5)
         add_b3(N - 1)
@@ -418,15 +445,13 @@ def tile_neuronpool_pa_kernel(tc, h1, W2, b2, W3, b3, gamma, beta, tick, out):
         finish(N - 6)
         spread(N - 4)
         centre(N - 5)
+        centre(N - 2)
         finish(N - 5)
         spread(N - 3)
         centre(N - 4)
-        finish(N - 4)
-        spread(N - 2)
-        centre(N - 3)
-        finish(N - 3)
-        spread(N - 1)
-        centre(N - 2)
-        finish(N - 2)
         centre(N - 1)
+        finish(N - 4)
+        centre(N - 3)
+        finish(N - 2)
+        finish(N - 3)
         finish(N - 1)

@@ -184,7 +184,7 @@ def tile_neuronpool_pa_kernel(tc, h1, W2, b2, W3, b3, gamma, beta, tick, out):
             quantise("x", n, tiles["x_grouped", n][:].rearrange("p b t -> p (b t)"), B)
 
         def scalar_runs(n):
-            return 80 + (108 - 80) * n // (N - 1) // 2 * 2
+            return 76 + (112 - 76) * n // (N - 1) // 2 * 2
 
         def regroup_w2_on_scalar(n):
             w2_grouped = make(work, "w2_grouped", n, [P, HID, PACK], BF16)
@@ -207,6 +207,10 @@ def tile_neuronpool_pa_kernel(tc, h1, W2, b2, W3, b3, gamma, beta, tick, out):
             nc.vector.tensor_copy(
                 out=words_in_runs(w3_grouped[:]), in_=rows_in_runs(tiles["w3_rows", n][:])
             )
+
+        def regroup_w3_on_scalar(n):
+            w3_grouped = make(work, "w3_grouped", n, [P, D, PACK], BF16)
+            nc.scalar.copy(out=words_in_runs(w3_grouped[:]), in_=rows_in_runs(tiles["w3_rows", n][:]))
 
         def quantise_w3(n):
             quantise("w3", n, tiles["w3_grouped", n][:].rearrange("p d t -> p (d t)"), D)
@@ -247,6 +251,26 @@ def tile_neuronpool_pa_kernel(tc, h1, W2, b2, W3, b3, gamma, beta, tick, out):
 
         def spread_late(n):
             spread(n, kind="hidden")
+
+        def spread_x(n):
+            spread(n, kind="x_turned")
+
+        def spread_early_0():
+            spread_x(N - 6)
+
+        def spread_early_1():
+            spread_x(N - 5)
+
+        def spread_b(n):
+            ln_all = psum_single.tile([P, 2, D], F32, name="b3_spread")
+            tiles["ln_all", n] = ln_all
+            for v in range(2):
+                for h in range(D_HALVES):
+                    nc.tensor.transpose(
+                        out=ln_all[:, v, h * P : (h + 1) * P],
+                        in_=ln_gain_cols[:, h, v, n : n + 1].to_broadcast([P, P]),
+                        identity=identity[:],
+                    )
 
         def quantise_g(n):
             quantise("g", n, tiles["g_grouped", n][:].rearrange("p b t -> p (b t)"), B)
@@ -320,11 +344,11 @@ def tile_neuronpool_pa_kernel(tc, h1, W2, b2, W3, b3, gamma, beta, tick, out):
                 accum_out=column("square_totals", n),
             )
 
-        def take_rstds(n):
+        def take_vars(n):
             first, size = GROUP_OF[n]
             if n != first + size - 1:
                 return
-            nc.gpsimd.tensor_scalar(
+            nc.vector.tensor_scalar(
                 out=make(work, "var_eps", first, [P, size], F32)[:],
                 in0=tiles["square_totals", first][:],
                 scalar1=1.0 / D**3,
@@ -332,6 +356,11 @@ def tile_neuronpool_pa_kernel(tc, h1, W2, b2, W3, b3, gamma, beta, tick, out):
                 op0=ALU.mult,
                 op1=ALU.add,
             )
+
+        def take_rstds(n):
+            first, size = GROUP_OF[n]
+            if n != first + size - 1:
+                return
             nc.gpsimd.tensor_tensor(
                 out=make(work, "rstds", first, [P, size], F32)[:],
                 in0=tiles["var_eps", first][:],
@@ -382,7 +411,6 @@ def tile_neuronpool_pa_kernel(tc, h1, W2, b2, W3, b3, gamma, beta, tick, out):
             run(first_layer, k - 1)
             run(turn_x, k + 3)
             run(spread_b3, k + 0)
-            run(spread, k - 8)
             run(regroup_w2_on_scalar, k + 1)
             run(copy_x, k + 2)
             run(copy_b3, k - 1)
@@ -391,67 +419,72 @@ def tile_neuronpool_pa_kernel(tc, h1, W2, b2, W3, b3, gamma, beta, tick, out):
             if k == -2:
                 turn_vectors()
             run(quantise_x, k + 0)
-            run(centre, k - 9)
             run(regroup_g, k - 2)
             run(quantise_w3, k - 2)
+            run(take_vars, k - 5)
             run(take_rstds, k - 5)
             run(regroup_w2_on_vector, k + 1)
+            run(finish, k - 9)
+            run(spread, k - 7)
+            if k == 30:
+                spread_early_0()
+            if k == 31:
+                spread_early_1()
             run(add_b3, k - 3)
+            run(centre, k - 8)
             run(take_means, k - 4)
             run(regroup_w3, k - 1)
             if k == -1:
                 keep_vectors()
-            run(finish, k - 9)
             run(quantise_g, k - 2)
             run(quantise_w2, k + 0)
 
         second_layer(N - 3)
         first_layer(N - 1)
-        spread(N - 8)
         sum_squares(N - 4)
         gelu(N - 1)
-        centre(N - 9)
+        regroup_w3_on_scalar(N - 1)
         regroup_g(N - 2)
-        quantise_w3(N - 2)
+        take_vars(N - 5)
         take_rstds(N - 5)
-        add_b3(N - 3)
-        sum_squares(N - 3)
-        regroup_w3(N - 1)
-        quantise_g(N - 2)
-        second_layer(N - 2)
+        quantise_w3(N - 2)
         finish(N - 9)
         spread(N - 7)
+        add_b3(N - 3)
         centre(N - 8)
+        sum_squares(N - 3)
+        quantise_g(N - 2)
+        second_layer(N - 2)
+        spread_b(N - 4)
+        finish(N - 8)
+        centre(N - 7)
         regroup_g(N - 1)
-        take_rstds(N - 3)
         take_means(N - 3)
+        take_vars(N - 3)
+        take_rstds(N - 3)
         quantise_w3(N - 1)
         add_b3(N - 2)
         sum_squares(N - 2)
         quantise_g(N - 1)
         second_layer(N - 1)
-        finish(N - 8)
-        spread(N - 6)
+        spread(N - 3)
         spread_late(N - 2)
         spread_late(N - 1)
-        centre(N - 7)
+        centre(N - 6)
         finish(N - 7)
-        spread(N - 5)
+        centre(N - 5)
         add_b3(N - 1)
         sum_squares(N - 1)
-        take_rstds(N - 1)
-        centre(N - 6)
-        take_means(N - 1)
         finish(N - 6)
-        spread(N - 4)
-        centre(N - 5)
-        centre(N - 2)
-        finish(N - 5)
-        spread(N - 3)
         centre(N - 4)
-        centre(N - 1)
-        finish(N - 4)
+        take_means(N - 1)
+        take_vars(N - 1)
+        take_rstds(N - 1)
+        finish(N - 5)
         centre(N - 3)
-        finish(N - 2)
+        finish(N - 4)
+        centre(N - 2)
         finish(N - 3)
+        centre(N - 1)
+        finish(N - 2)
         finish(N - 1)

from contextlib import ExitStack

import concourse.mybir as mybir
from concourse.masks import make_identity

FP8X4 = mybir.dt.float8_e4m3fn_x4
BF16 = mybir.dt.bfloat16
F32 = mybir.dt.float32
U32 = mybir.dt.uint32
U8 = mybir.dt.uint8
ALU = mybir.AluOpType
ACT = mybir.ActivationFunctionType

P = 128
PACK = 4
B, N, HID, D = 128, 32, 512, 256
D_HALVES = D // P
LN_EPS = 1e-5
FMIN, FMAX, TICK_INTERVAL = 0.5, 40.0, 0.1
PI = 3.141592653589793
SINE_TERMS = 16

RUN = 4
W2_SCALAR_RUNS = 106
W2_SCALAR_RUNS_FIRST = 64
FIRST_STEP = -3
LOADS_AHEAD = 4
B3_GROUP = 4
LOAD_BUFS = LOADS_AHEAD + 4

GROUP_SIZES = [4] * 7 + [2] * 2
GROUP_OF = [(sum(GROUP_SIZES[:g]), size) for g, size in enumerate(GROUP_SIZES) for j in range(size)]

FLOPS = 2 * B * N * HID * (HID + D)


def sine(angle):
    x = (angle + PI) % (2.0 * PI) - PI
    term, total = x, x
    for k in range(1, SINE_TERMS):
        term = -term * x * x / ((2 * k) * (2 * k + 1))
        total = total + term
    return total


def oscillator_gain(n, tick):
    freq = FMIN * (FMAX / FMIN) ** (n / (N - 1))
    phase = (n * 2.3571) % (2.0 * PI)
    return 1.0 + 0.5 * sine(2.0 * PI * freq * tick * TICK_INTERVAL + phase)


def rows_in_runs(rows):
    return rows.rearrange("p t (c i) -> p c t i", i=RUN)


def words_in_runs(grouped):
    return grouped.rearrange("p (c i) t -> p c t i", i=RUN)


def tile_neuronpool_pa_kernel(tc, h1, W2, b2, W3, b3, gamma, beta, tick, out):
    nc = tc.nc
    with ExitStack() as stack:
        consts = stack.enter_context(tc.tile_pool(name="consts", bufs=1))
        loads = stack.enter_context(tc.tile_pool(name="loads", bufs=LOAD_BUFS))
        work = stack.enter_context(tc.tile_pool(name="work", bufs=4))
        ln = stack.enter_context(tc.tile_pool(name="ln", bufs=8))
        psum_pairs = stack.enter_context(tc.psum_pool(name="psum_pairs", bufs=2))
        psum_single = stack.enter_context(tc.psum_pool(name="psum_single", bufs=1))
        stack.enter_context(tc.manual_schedule())

        tiles = {}

        def make(pool, name, n, shape, dtype):
            tiles[name, n] = pool.tile(shape, dtype, name=name, align_bytes=64)
            return tiles[name, n]

        def make_bank(pool, name, n, shape):
            tiles[name, n] = pool.tile(shape, F32, name=name)
            return tiles[name, n]

        identity = consts.tile([P, P], F32)
        make_identity(nc, identity[:])
        identity_bf16 = consts.tile([P, P], BF16)
        nc.gpsimd.tensor_copy(out=identity_bf16[:], in_=identity[:])
        minus_half = consts.tile([P, max(GROUP_SIZES)], F32)
        nc.vector.memset(minus_half[:], -0.5)
        ones = consts.tile([P, 1], F32)
        nc.vector.memset(ones[:], 1.0)

        b2_rows = consts.tile([P, HID], BF16)
        nc.vector.memset(b2_rows[:], 0.0)
        ln_rows = consts.tile([P, D], BF16)
        nc.vector.memset(ln_rows[:], 0.0)
        b2_cols = consts.tile([P, PACK, N], F32)
        ln_gain_cols = consts.tile([P, D_HALVES, 2, N], F32)
        b3_cols = consts.tile([P, D_HALVES, N], BF16)
        gains = consts.tile([P, N], F32)
        nc.scalar.activation(out=gains[:, 0:1], in_=ones[:], func=ACT.Gelu, bias=0.0, scale=1.0)
        for n in range(N):
            nc.scalar.mul(out=gains[:, n : n + 1], in_=ones[:], mul=oscillator_gain(n, tick))

        def load_vectors():
            nc.sync.dma_start(out=b2_rows[0:N, :], in_=b2)
            for v, vector in enumerate((gamma, beta, b3)):
                nc.sync.dma_start(out=ln_rows[v * N : (v + 1) * N, :], in_=vector)

        def load_x(n):
            if n % 2 == 0:
                x_rows = make(loads, "x_rows", n, [P, 2, HID], BF16)
                nc.sync.dma_start(out=x_rows[:], in_=h1[:, n : n + 2, :])

        def load_w2(n):
            w2_rows = make(loads, "w2_rows", n, [P, PACK, HID], BF16)
            nc.sync.dma_start(out=w2_rows[:].rearrange("p (u e) j -> p u e j", u=2), in_=W2[n].rearrange("(u p e) j -> p u e j", u=2, e=2))

        def load_w3(n):
            w3_rows = make(loads, "w3_rows", n, [P, PACK, D], BF16)
            nc.sync.dma_start(out=w3_rows[:], in_=W3[n].rearrange("(t p) d -> p t d", p=P))

        load_x(0)
        load_w2(0)
        load_vectors()
        load_x(1)
        load_w2(1)
        load_x(2)
        load_w2(2)
        load_x(3)
        load_w3(0)
        load_w2(3)
        load_x(4)
        load_w3(1)

        def turn_vectors():
            b2_rows_f32 = consts.tile([P, PACK, P], F32)
            nc.vector.tensor_copy(out=b2_rows_f32[:], in_=b2_rows[:].rearrange("n (t p) -> n t p", p=P))
            tiles["b2_turned"] = psum_pairs.tile([P, PACK, P], F32, name="hidden")
            for t in range(PACK):
                nc.tensor.transpose(
                    out=tiles["b2_turned"][:, t, :], in_=b2_rows_f32[:, t, :], identity=identity[:]
                )
            ln_rows_f32 = consts.tile([P, D], F32)
            nc.vector.tensor_copy(out=ln_rows_f32[:], in_=ln_rows[:])
            tiles["ln_turned"] = psum_pairs.tile([P, D_HALVES, P], F32, name="ln_all")
            for h in range(D_HALVES):
                nc.tensor.transpose(
                    out=tiles["ln_turned"][:, h, :],
                    in_=ln_rows_f32[:, h * P : (h + 1) * P],
                    identity=identity[:],
                )

        def keep_vectors():
            nc.vector.tensor_copy(out=b2_cols[:], in_=tiles["b2_turned"][:, :, 0:N])
            ln_by_vector = tiles["ln_turned"][:].rearrange("p h (v n) -> p h v n", n=N)
            nc.vector.tensor_copy(out=b3_cols[:], in_=ln_by_vector[:, :, 2, :])
            for v in range(2):
                nc.vector.tensor_tensor(
                    out=ln_gain_cols[:, :, v, :],
                    in0=ln_by_vector[:, :, v, :],
                    in1=gains[:].unsqueeze(1).to_broadcast([P, D_HALVES, N]),
                    op=ALU.mult,
                )

        def quantise(name, n, grouped, width):
            codes = make(work, name + "_codes", n, [P, width], U32)
            scales = make(work, name + "_scales", n, [P, width], U8)
            nc.vector.quantize_mx(out=codes[:].bitcast(FP8X4), scales=scales[:], in_=grouped)

        def turn_x(n):
            x_words = tiles["x_rows", n - n % 2][:, n % 2, :].bitcast(F32).rearrange("b (u p) -> b u p", u=2)
            x_turned = make_bank(psum_pairs, "x_turned", n, [P, 2, B])
            for u in range(2):
                nc.tensor.transpose(out=x_turned[:, u, :], in_=x_words[:, u, :], identity=identity[:])

        def copy_x(n):
            x_grouped = make(work, "x_grouped", n, [P, B, PACK], BF16)
            nc.scalar.copy(
                out=x_grouped[:].rearrange("p b t -> p (b t)").bitcast(F32).rearrange(
                    "p (b u) -> p b u", u=2
                ),
                in_=tiles["x_turned", n][:].rearrange("p u b -> p b u"),
            )

        def quantise_x(n):
            quantise("x", n, tiles["x_grouped", n][:].rearrange("p b t -> p (b t)"), B)

        def scalar_runs(n):
            return 76 + (112 - 76) * n // (N - 1) // 2 * 2

        def regroup_w2_on_scalar(n):
            w2_grouped = make(work, "w2_grouped", n, [P, HID, PACK], BF16)
            nc.scalar.copy(
                out=words_in_runs(w2_grouped[:])[:, : scalar_runs(n)],
                in_=rows_in_runs(tiles["w2_rows", n][:])[:, : scalar_runs(n)],
            )

        def regroup_w2_on_vector(n):
            nc.vector.tensor_copy(
                out=words_in_runs(tiles["w2_grouped", n][:])[:, scalar_runs(n) :],
                in_=rows_in_runs(tiles["w2_rows", n][:])[:, scalar_runs(n) :],
            )

        def quantise_w2(n):
            quantise("w2", n, tiles["w2_grouped", n][:].rearrange("p j t -> p (j t)"), HID)

        def regroup_w3(n):
            w3_grouped = make(work, "w3_grouped", n, [P, D, PACK], BF16)
            nc.vector.tensor_copy(
                out=words_in_runs(w3_grouped[:]), in_=rows_in_runs(tiles["w3_rows", n][:])
            )

        def regroup_w3_on_scalar(n):
            w3_grouped = make(work, "w3_grouped", n, [P, D, PACK], BF16)
            nc.scalar.copy(out=words_in_runs(w3_grouped[:]), in_=rows_in_runs(tiles["w3_rows", n][:]))

        def quantise_w3(n):
            quantise("w3", n, tiles["w3_grouped", n][:].rearrange("p d t -> p (d t)"), D)

        def first_layer(n):
            hidden = make_bank(psum_pairs, "hidden", n, [P, PACK, B])
            for t in range(PACK):
                nc.tensor.matmul_mx(
                    out=hidden[:, t, :],
                    lhsT=tiles["w2_codes", n][:, t * P : (t + 1) * P].bitcast(FP8X4),
                    lhsT_scale=tiles["w2_scales", n][:, t * P : (t + 1) * P],
                    rhs=tiles["x_codes", n][:].bitcast(FP8X4),
                    rhs_scale=tiles["x_scales", n][:],
                    start=True,
                    stop=True,
                )

        def gelu(n):
            g_rows = make(work, "g_rows", n, [P, PACK, B], BF16)
            for t in range(PACK):
                nc.scalar.activation(
                    out=g_rows[:, t, :],
                    in_=tiles["hidden", n][:, t, :],
                    func=ACT.Gelu,
                    bias=b2_cols[:, t, n : n + 1],
                    scale=1.0,
                )

        def regroup_g(n):
            g_grouped = make(work, "g_grouped", n, [P, B, PACK], BF16)
            nc.vector.tensor_copy(
                out=words_in_runs(g_grouped[:]), in_=rows_in_runs(tiles["g_rows", n][:])
            )

        def regroup_g_on_scalar(n):
            g_grouped = make(work, "g_grouped", n, [P, B, PACK], BF16)
            nc.scalar.copy(out=words_in_runs(g_grouped[:]), in_=rows_in_runs(tiles["g_rows", n][:]))

        def spread_late(n):
            spread(n, kind="hidden")

        def spread_x(n):
            spread(n, kind="x_turned")

        def spread_early_0():
            spread_x(N - 6)

        def spread_early_1():
            spread_x(N - 5)

        def spread_b(n):
            ln_all = psum_single.tile([P, 2, D], F32, name="b3_spread")
            tiles["ln_all", n] = ln_all
            for v in range(2):
                for h in range(D_HALVES):
                    nc.tensor.transpose(
                        out=ln_all[:, v, h * P : (h + 1) * P],
                        in_=ln_gain_cols[:, h, v, n : n + 1].to_broadcast([P, P]),
                        identity=identity[:],
                    )

        def quantise_g(n):
            quantise("g", n, tiles["g_grouped", n][:].rearrange("p b t -> p (b t)"), B)

        def second_layer(n):
            y_sums = make_bank(psum_single, "y_sums", n, [P, D])
            nc.tensor.matmul_mx(
                out=y_sums[:],
                lhsT=tiles["g_codes", n][:].bitcast(FP8X4),
                lhsT_scale=tiles["g_scales", n][:],
                rhs=tiles["w3_codes", n][:].bitcast(FP8X4),
                rhs_scale=tiles["w3_scales", n][:],
                start=True,
                stop=True,
            )

        def spread_b3(n):
            if n % B3_GROUP == 0:
                b3_spread = psum_single.tile([P, B3_GROUP, D], BF16, name="b3_spread")
                tiles["b3_spread", n] = b3_spread
                for j in range(B3_GROUP):
                    for h in range(D_HALVES):
                        nc.tensor.transpose(
                            out=b3_spread[:, j, h * P : (h + 1) * P],
                            in_=b3_cols[:, h, n + j : n + j + 1].to_broadcast([P, P]),
                            identity=identity_bf16[:],
                        )

        def copy_b3(n):
            if n % B3_GROUP == 0:
                b3_all = make(work, "b3_all", n, [P, B3_GROUP, D], BF16)
                nc.scalar.copy(out=b3_all[:], in_=tiles["b3_spread", n][:])

        def spread(n, kind="ln_all"):
            ln_all = psum_pairs.tile([P, 2, D], F32, name=kind)
            tiles["ln_all", n] = ln_all
            for v in range(2):
                for h in range(D_HALVES):
                    nc.tensor.transpose(
                        out=ln_all[:, v, h * P : (h + 1) * P],
                        in_=ln_gain_cols[:, h, v, n : n + 1].to_broadcast([P, P]),
                        identity=identity[:],
                    )

        def column(name, n):
            first, size = GROUP_OF[n]
            return tiles[name, first][:, n - first : n - first + 1]

        def add_b3(n):
            first, size = GROUP_OF[n]
            if n == first:
                make(work, "y_totals", first, [P, size], F32)
                make(work, "square_totals", first, [P, size], F32)
            nc.vector.scalar_tensor_tensor(
                out=make(ln, "y", n, [P, D], F32)[:],
                in0=tiles["y_sums", n][:],
                scalar=1.0,
                in1=tiles["b3_all", n - n % B3_GROUP][:, n % B3_GROUP, :],
                op0=ALU.mult,
                op1=ALU.add,
                accum_out=column("y_totals", n),
            )

        def sum_squares(n):
            nc.scalar.activation(
                out=make(work, "squares", n, [P, D], F32)[:],
                in_=tiles["y", n][:],
                func=ACT.Square,
                bias=column("y_totals", n),
                scale=-float(D),
                accum_out=column("square_totals", n),
            )

        def take_vars(n):
            first, size = GROUP_OF[n]
            if n != first + size - 1:
                return
            nc.vector.tensor_scalar(
                out=make(work, "var_eps", first, [P, size], F32)[:],
                in0=tiles["square_totals", first][:],
                scalar1=1.0 / D**3,
                scalar2=LN_EPS,
                op0=ALU.mult,
                op1=ALU.add,
            )

        def take_rstds(n):
            first, size = GROUP_OF[n]
            if n != first + size - 1:
                return
            nc.gpsimd.tensor_tensor(
                out=make(work, "rstds", first, [P, size], F32)[:],
                in0=tiles["var_eps", first][:],
                in1=minus_half[:, 0:size],
                op=ALU.pow,
            )

        def take_means(n):
            first, size = GROUP_OF[n]
            if n == first + size - 1:
                nc.vector.tensor_scalar_mul(
                    out=make(work, "means", first, [P, size], F32)[:],
                    in0=tiles["y_totals", first][:],
                    scalar1=1.0 / D,
                )

        def centre(n):
            nc.vector.scalar_tensor_tensor(
                out=make(work, "centred", n, [P, D], F32)[:],
                in0=tiles["y", n][:],
                scalar=column("means", n),
                in1=tiles["ln_all", n][:, 0, :],
                op0=ALU.subtract,
                op1=ALU.mult,
            )

        def finish(n):
            result = make(ln, "result", n, [P, D], F32)
            nc.vector.scalar_tensor_tensor(
                out=result[:],
                in0=tiles["centred", n][:],
                scalar=column("rstds", n),
                in1=tiles["ln_all", n][:, 1, :],
                op0=ALU.mult,
                op1=ALU.add,
            )
            nc.sync.dma_start(out=out[:, n, :], in_=result[:])

        def run(stage, n):
            if 0 <= n < N:
                stage(n)

        for k in range(FIRST_STEP, N):
            run(load_x, k + 8)
            run(load_w2, k + 7)
            run(load_w3, k + 5)
            run(second_layer, k - 3)
            run(first_layer, k - 1)
            run(turn_x, k + 3)
            run(spread_b3, k + 0)
            run(regroup_w2_on_scalar, k + 1)
            run(copy_x, k + 2)
            run(copy_b3, k - 1)
            run(sum_squares, k - 4)
            run(gelu, k - 1)
            if k == -2:
                turn_vectors()
            run(quantise_x, k + 0)
            run(regroup_g, k - 2)
            run(quantise_w3, k - 2)
            run(take_vars, k - 5)
            run(take_rstds, k - 5)
            run(regroup_w2_on_vector, k + 1)
            run(finish, k - 9)
            run(spread, k - 7)
            if k == 30:
                spread_early_0()
            if k == 31:
                spread_early_1()
            run(add_b3, k - 3)
            run(centre, k - 8)
            run(take_means, k - 4)
            run(regroup_w3, k - 1)
            if k == -1:
                keep_vectors()
            run(quantise_g, k - 2)
            run(quantise_w2, k + 0)

        second_layer(N - 3)
        first_layer(N - 1)
        sum_squares(N - 4)
        gelu(N - 1)
        regroup_w3_on_scalar(N - 1)
        regroup_g(N - 2)
        take_vars(N - 5)
        take_rstds(N - 5)
        quantise_w3(N - 2)
        finish(N - 9)
        spread(N - 7)
        add_b3(N - 3)
        centre(N - 8)
        sum_squares(N - 3)
        quantise_g(N - 2)
        second_layer(N - 2)
        spread_b(N - 4)
        finish(N - 8)
        centre(N - 7)
        regroup_g(N - 1)
        take_means(N - 3)
        take_vars(N - 3)
        take_rstds(N - 3)
        quantise_w3(N - 1)
        add_b3(N - 2)
        sum_squares(N - 2)
        quantise_g(N - 1)
        second_layer(N - 1)
        spread(N - 3)
        spread_late(N - 2)
        spread_late(N - 1)
        centre(N - 6)
        finish(N - 7)
        centre(N - 5)
        add_b3(N - 1)
        sum_squares(N - 1)
        finish(N - 6)
        centre(N - 4)
        take_means(N - 1)
        take_vars(N - 1)
        take_rstds(N - 1)
        finish(N - 5)
        centre(N - 3)
        finish(N - 4)
        centre(N - 2)
        finish(N - 3)
        centre(N - 1)
        finish(N - 2)
        finish(N - 1)
